import numpy as np
import ml_dtypes

BF16 = ml_dtypes.bfloat16


def bf(x):
    return np.asarray(x, np.float32).astype(BF16)


def f32(x):
    return np.asarray(x, np.float32)


def f64(x):
    return np.asarray(x).astype(np.float64)


def striped(idx):
    return np.tile(idx.reshape(-1, 16).T, (8, 1))


C, S, K, N = 128, 4096, 2, 8192


def setup_inputs():
    return {"x": f32(np.random.uniform(size=(C, S))), "field": f32(2.0 * np.random.standard_normal((1, S)) / np.sqrt(S)), "coup": f32(3.0 * np.random.standard_normal((1, N)) / np.sqrt(N)), "bias": f32(1.0 + 0.1 * np.random.standard_normal(1)), "offs": striped(np.concatenate([np.random.permutation(S) for _ in range(K)]))}


def reference(x, field, coup, bias, offs):
    idx = offs[:16].T.reshape(-1)
    xs = f64(x)
    single = (xs * f64(field)).sum(axis=1, keepdims=True)
    pair = (xs[:, idx] * f64(coup) * np.tile(xs, (1, K))).sum(axis=1, keepdims=True)
    return single + pair + f64(bias)[0]

@@ -1,0 +1,78 @@
+import concourse.mybir as mybir
+from concourse.masks import make_identity
+
+F32 = mybir.dt.float32
+U16 = mybir.dt.uint16
+MULT = mybir.AluOpType.mult
+IDENTITY = mybir.ActivationFunctionType.Identity
+
+C = 128
+S = 4096
+N = 8192
+PIECE = 1024
+LINEAR_PIECES = S // PIECE
+PAIR_PIECES = N // PIECE
+
+FLOPS = C * (2 * S + 3 * N)
+
+
+def tile_linearpairwisemodule_kernel(tc, x, field, coup, bias, offs, out):
+    nc = tc.nc
+    field_row = field.rearrange("o s -> (o s)")
+    coup_row = coup.rearrange("o n -> (o n)")
+    with (
+        tc.tile_pool(name="held", bufs=1) as held,
+        tc.tile_pool(name="stream", bufs=3) as stream,
+        tc.psum_pool(name="psum", bufs=1) as psum,
+    ):
+        offsets = held.tile([C, N // 16], U16, name="offsets")
+        nc.sync.dma_start(offsets[:], offs)
+
+        table = held.tile([C, S], F32, name="table")
+        for p in range(LINEAR_PIECES):
+            cols = slice(p * PIECE, (p + 1) * PIECE)
+            nc.sync.dma_start(table[:, cols], x[:, cols])
+
+        bias_one = held.tile([1, 1], F32, name="bias_one")
+        nc.sync.dma_start(bias_one[:], bias.unsqueeze(0))
+
+        identity = held.tile([C, C], F32, name="identity")
+        make_identity(nc, identity[:])
+
+        sums = held.tile([C, LINEAR_PIECES + PAIR_PIECES], F32, name="sums")
+        energy_row = psum.tile([1, C], F32, name="energy_row")
+
+        def add_up(products, k):
+            spent = stream.tile([C, PIECE], F32, name="spent")
+            nc.scalar.activation(spent[:], products[:], IDENTITY, accum_out=sums[:, k : k + 1])
+            nc.tensor.matmul(
+                energy_row[:],
+                sums[:, k : k + 1],
+                identity[:],
+                start=(k == 0),
+                stop=(k == LINEAR_PIECES + PAIR_PIECES - 1),
+            )
+
+        for p in range(LINEAR_PIECES):
+            cols = slice(p * PIECE, (p + 1) * PIECE)
+            field_all = stream.tile([C, PIECE], F32, name="field_all")
+            nc.sync.dma_start(field_all[:], field_row[cols].partition_broadcast(C))
+            linear = stream.tile([C, PIECE], F32, name="linear")
+            nc.vector.tensor_tensor(linear[:], table[:, cols], field_all[:], MULT)
+            add_up(linear, p)
+
+        for p in range(PAIR_PIECES):
+            pairs = slice(p * PIECE, (p + 1) * PIECE)
+            first = (p * PIECE) % S
+            coup_all = stream.tile([C, PIECE], F32, name="coup_all")
+            nc.sync.dma_start(coup_all[:], coup_row[pairs].partition_broadcast(C))
+            partner = stream.tile([C, PIECE], F32, name="partner")
+            nc.vector.tensor_tensor(partner[:], table[:, first : first + PIECE], coup_all[:], MULT)
+            pairwise = stream.tile([C, PIECE], F32, name="pairwise")
+            picked = table[:].indirect(offsets[:, p * (PIECE // 16) : (p + 1) * (PIECE // 16)])
+            nc.vector.tensor_tensor(pairwise[:], picked, partner[:], MULT)
+            add_up(pairwise, LINEAR_PIECES + p)
+
+        energy = held.tile([1, C], F32, name="energy")
+        nc.vector.tensor_scalar_add(energy[:], energy_row[:], bias_one[:, 0:1])
+        nc.sync.dma_start(out.rearrange("c o -> o c"), energy[:])

@@ -10,68 +10,98 @@ C = 128
 S = 4096
 N = 8192
 PIECE = 1024
-LINEAR_PIECES = S // PIECE
-PAIR_PIECES = N // PIECE
+PIECES = N // PIECE
+BLOCK = 128
+BLOCKS = S // BLOCK
+BANK = 512
+BLOCKS_IN_BANK = BANK // BLOCK
 
 FLOPS = C * (2 * S + 3 * N)
 
 
 def tile_linearpairwisemodule_kernel(tc, x, field, coup, bias, offs, out):
     nc = tc.nc
-    field_row = field.rearrange("o s -> (o s)")
     coup_row = coup.rearrange("o n -> (o n)")
     with (
         tc.tile_pool(name="held", bufs=1) as held,
         tc.tile_pool(name="stream", bufs=3) as stream,
         tc.psum_pool(name="psum", bufs=1) as psum,
+        tc.psum_pool(name="banks", bufs=2) as banks,
     ):
-        offsets = held.tile([C, N // 16], U16, name="offsets")
-        nc.sync.dma_start(offsets[:], offs)
+        field_rows = held.tile([BLOCKS, BLOCK], F32, name="field_rows")
+        nc.sync.dma_start(field_rows[:], field.rearrange("o (b s) -> (o b) s", s=BLOCK))
+        bias_one = held.tile([1, 1], F32, name="bias_one")
+        nc.sync.dma_start(bias_one[:], bias.unsqueeze(0))
 
         table = held.tile([C, S], F32, name="table")
-        for p in range(LINEAR_PIECES):
+        coup_all = held.tile([C, N], F32, name="coup_all")
+        offsets = held.tile([C, N // 16], U16, name="offsets")
+
+        def load_table(p):
             cols = slice(p * PIECE, (p + 1) * PIECE)
             nc.sync.dma_start(table[:, cols], x[:, cols])
 
-        bias_one = held.tile([1, 1], F32, name="bias_one")
-        nc.sync.dma_start(bias_one[:], bias.unsqueeze(0))
+        def load_coup(p):
+            cols = slice(p * PIECE, (p + 1) * PIECE)
+            nc.sync.dma_start(coup_all[:, cols], coup_row[cols].partition_broadcast(C))
+
+        load_table(0)
+        load_coup(0)
+        for p in range(1, S // PIECE):
+            load_table(p)
+        nc.sync.dma_start(offsets[:], offs)
+        for p in range(1, PIECES):
+            load_coup(p)
 
         identity = held.tile([C, C], F32, name="identity")
         make_identity(nc, identity[:])
 
-        sums = held.tile([C, LINEAR_PIECES + PAIR_PIECES], F32, name="sums")
         energy_row = psum.tile([1, C], F32, name="energy_row")
 
-        def add_up(products, k):
-            spent = stream.tile([C, PIECE], F32, name="spent")
-            nc.scalar.activation(spent[:], products[:], IDENTITY, accum_out=sums[:, k : k + 1])
-            nc.tensor.matmul(
-                energy_row[:],
-                sums[:, k : k + 1],
-                identity[:],
-                start=(k == 0),
-                stop=(k == LINEAR_PIECES + PAIR_PIECES - 1),
-            )
+        field_cols_ps = psum.tile([BLOCK, BLOCKS], F32, name="field_cols_ps")
+        nc.tensor.matmul(
+            field_cols_ps[:], field_rows[:], identity[0:BLOCKS, 0:BLOCKS], start=True, stop=True
+        )
+        field_cols = held.tile([BLOCK, BLOCKS], F32, name="field_cols")
+        nc.scalar.activation(field_cols[:], field_cols_ps[:], IDENTITY)
 
-        for p in range(LINEAR_PIECES):
-            cols = slice(p * PIECE, (p + 1) * PIECE)
-            field_all = stream.tile([C, PIECE], F32, name="field_all")
-            nc.sync.dma_start(field_all[:], field_row[cols].partition_broadcast(C))
-            linear = stream.tile([C, PIECE], F32, name="linear")
-            nc.vector.tensor_tensor(linear[:], table[:, cols], field_all[:], MULT)
-            add_up(linear, p)
+        for g in range(BLOCKS // BLOCKS_IN_BANK):
+            flipped_ps = banks.tile([BLOCK, BANK], F32, name="flipped_ps")
+            for i in range(BLOCKS_IN_BANK):
+                b = g * BLOCKS_IN_BANK + i
+                nc.tensor.transpose(
+                    flipped_ps[:, i * BLOCK : (i + 1) * BLOCK],
+                    table[:, b * BLOCK : (b + 1) * BLOCK],
+                    identity[:],
+                )
+            flipped = stream.tile([BLOCK, BANK], F32, name="flipped")
+            nc.scalar.activation(flipped[:], flipped_ps[:], IDENTITY)
+            for i in range(BLOCKS_IN_BANK):
+                b = g * BLOCKS_IN_BANK + i
+                nc.tensor.matmul(
+                    energy_row[:],
+                    field_cols[:, b : b + 1],
+                    flipped[:, i * BLOCK : (i + 1) * BLOCK],
+                    start=(b == 0),
+                    stop=False,
+                )
 
-        for p in range(PAIR_PIECES):
+        sums = held.tile([C, PIECES], F32, name="sums")
+        for p in range(PIECES):
             pairs = slice(p * PIECE, (p + 1) * PIECE)
             first = (p * PIECE) % S
-            coup_all = stream.tile([C, PIECE], F32, name="coup_all")
-            nc.sync.dma_start(coup_all[:], coup_row[pairs].partition_broadcast(C))
             partner = stream.tile([C, PIECE], F32, name="partner")
-            nc.vector.tensor_tensor(partner[:], table[:, first : first + PIECE], coup_all[:], MULT)
-            pairwise = stream.tile([C, PIECE], F32, name="pairwise")
+            nc.vector.tensor_tensor(
+                partner[:], table[:, first : first + PIECE], coup_all[:, pairs], MULT
+            )
             picked = table[:].indirect(offsets[:, p * (PIECE // 16) : (p + 1) * (PIECE // 16)])
+            pairwise = stream.tile([C, PIECE], F32, name="pairwise")
             nc.vector.tensor_tensor(pairwise[:], picked, partner[:], MULT)
-            add_up(pairwise, LINEAR_PIECES + p)
+            spent = stream.tile([C, PIECE], F32, name="spent")
+            nc.scalar.activation(spent[:], pairwise[:], IDENTITY, accum_out=sums[:, p : p + 1])
+            nc.tensor.matmul(
+                energy_row[:], sums[:, p : p + 1], identity[:], start=False, stop=(p == PIECES - 1)
+            )
 
         energy = held.tile([1, C], F32, name="energy")
         nc.vector.tensor_scalar_add(energy[:], energy_row[:], bias_one[:, 0:1])

@@ -4,6 +4,7 @@ from concourse.masks import make_identity
 F32 = mybir.dt.float32
 U16 = mybir.dt.uint16
 MULT = mybir.AluOpType.mult
+ADD = mybir.AluOpType.add
 IDENTITY = mybir.ActivationFunctionType.Identity
 
 C = 128
@@ -56,8 +57,7 @@ def tile_linearpairwisemodule_kernel(tc, x, field, coup, bias, offs, out):
         identity = held.tile([C, C], F32, name="identity")
         make_identity(nc, identity[:])
 
-        energy_row = psum.tile([1, C], F32, name="energy_row")
-
+        linear_row = psum.tile([1, C], F32, name="linear_row")
         field_cols_ps = psum.tile([BLOCK, BLOCKS], F32, name="field_cols_ps")
         nc.tensor.matmul(
             field_cols_ps[:], field_rows[:], identity[0:BLOCKS, 0:BLOCKS], start=True, stop=True
@@ -79,19 +79,22 @@ def tile_linearpairwisemodule_kernel(tc, x, field, coup, bias, offs, out):
             for i in range(BLOCKS_IN_BANK):
                 b = g * BLOCKS_IN_BANK + i
                 nc.tensor.matmul(
-                    energy_row[:],
+                    linear_row[:],
                     field_cols[:, b : b + 1],
                     flipped[:, i * BLOCK : (i + 1) * BLOCK],
                     start=(b == 0),
-                    stop=False,
+                    stop=(b == BLOCKS - 1),
                 )
+        linear_and_bias = held.tile([1, C], F32, name="linear_and_bias")
+        nc.scalar.activation(linear_and_bias[:], linear_row[:], IDENTITY, bias=bias_one[:, 0:1])
 
         sums = held.tile([C, PIECES], F32, name="sums")
+        pair_row = psum.tile([1, C], F32, name="pair_row")
         for p in range(PIECES):
             pairs = slice(p * PIECE, (p + 1) * PIECE)
             first = (p * PIECE) % S
             partner = stream.tile([C, PIECE], F32, name="partner")
-            nc.vector.tensor_tensor(
+            nc.gpsimd.tensor_tensor(
                 partner[:], table[:, first : first + PIECE], coup_all[:, pairs], MULT
             )
             picked = table[:].indirect(offsets[:, p * (PIECE // 16) : (p + 1) * (PIECE // 16)])
@@ -100,9 +103,9 @@ def tile_linearpairwisemodule_kernel(tc, x, field, coup, bias, offs, out):
             spent = stream.tile([C, PIECE], F32, name="spent")
             nc.scalar.activation(spent[:], pairwise[:], IDENTITY, accum_out=sums[:, p : p + 1])
             nc.tensor.matmul(
-                energy_row[:], sums[:, p : p + 1], identity[:], start=False, stop=(p == PIECES - 1)
+                pair_row[:], sums[:, p : p + 1], identity[:], start=(p == 0), stop=(p == PIECES - 1)
             )
 
         energy = held.tile([1, C], F32, name="energy")
-        nc.vector.tensor_scalar_add(energy[:], energy_row[:], bias_one[:, 0:1])
+        nc.vector.tensor_tensor(energy[:], pair_row[:], linear_and_bias[:], ADD)
         nc.sync.dma_start(out.rearrange("c o -> o c"), energy[:])

@@ -4,7 +4,6 @@ from concourse.masks import make_identity
 F32 = mybir.dt.float32
 U16 = mybir.dt.uint16
 MULT = mybir.AluOpType.mult
-ADD = mybir.AluOpType.add
 IDENTITY = mybir.ActivationFunctionType.Identity
 
 C = 128
@@ -13,9 +12,12 @@ N = 8192
 PIECE = 1024
 PIECES = N // PIECE
 BLOCK = 128
-BLOCKS = S // BLOCK
 BANK = 512
 BLOCKS_IN_BANK = BANK // BLOCK
+FIELD_BLOCKS = S // BLOCK
+PIECE_BLOCKS = PIECE // BLOCK
+TENSOR_PIECES = 2
+WEIGHT_BLOCKS = FIELD_BLOCKS + TENSOR_PIECES * PIECE_BLOCKS
 
 FLOPS = C * (2 * S + 3 * N)
 
@@ -23,89 +25,100 @@ FLOPS = C * (2 * S + 3 * N)
 def tile_linearpairwisemodule_kernel(tc, x, field, coup, bias, offs, out):
     nc = tc.nc
     coup_row = coup.rearrange("o n -> (o n)")
+    coup_blocks = coup.rearrange("o (b s) -> (o b) s", s=BLOCK)
     with (
         tc.tile_pool(name="held", bufs=1) as held,
         tc.tile_pool(name="stream", bufs=3) as stream,
+        tc.tile_pool(name="product_pool", bufs=TENSOR_PIECES + 3) as product_pool,
         tc.psum_pool(name="psum", bufs=1) as psum,
         tc.psum_pool(name="banks", bufs=2) as banks,
     ):
-        field_rows = held.tile([BLOCKS, BLOCK], F32, name="field_rows")
-        nc.sync.dma_start(field_rows[:], field.rearrange("o (b s) -> (o b) s", s=BLOCK))
+        weight_rows = held.tile([WEIGHT_BLOCKS, BLOCK], F32, name="weight_rows")
+        nc.sync.dma_start(
+            weight_rows[0:FIELD_BLOCKS, :], field.rearrange("o (b s) -> (o b) s", s=BLOCK)
+        )
+        nc.sync.dma_start(
+            weight_rows[FIELD_BLOCKS:WEIGHT_BLOCKS, :], coup_blocks[0 : TENSOR_PIECES * PIECE_BLOCKS, :]
+        )
         bias_one = held.tile([1, 1], F32, name="bias_one")
         nc.sync.dma_start(bias_one[:], bias.unsqueeze(0))
 
         table = held.tile([C, S], F32, name="table")
-        coup_all = held.tile([C, N], F32, name="coup_all")
-        offsets = held.tile([C, N // 16], U16, name="offsets")
-
-        def load_table(p):
+        for p in range(S // PIECE):
             cols = slice(p * PIECE, (p + 1) * PIECE)
             nc.sync.dma_start(table[:, cols], x[:, cols])
-
-        def load_coup(p):
+        offsets = held.tile([C, N // 16], U16, name="offsets")
+        nc.sync.dma_start(offsets[:], offs)
+        coup_all = held.tile([C, N], F32, name="coup_all")
+        for p in range(TENSOR_PIECES, PIECES):
             cols = slice(p * PIECE, (p + 1) * PIECE)
             nc.sync.dma_start(coup_all[:, cols], coup_row[cols].partition_broadcast(C))
 
-        load_table(0)
-        load_coup(0)
-        for p in range(1, S // PIECE):
-            load_table(p)
-        nc.sync.dma_start(offsets[:], offs)
-        for p in range(1, PIECES):
-            load_coup(p)
+        partners = held.tile([C, S], F32, name="partners")
+        for p in range(S // PIECE):
+            cols = slice(p * PIECE, (p + 1) * PIECE)
+            nc.scalar.activation(partners[:, cols], table[:, cols], IDENTITY)
 
         identity = held.tile([C, C], F32, name="identity")
         make_identity(nc, identity[:])
 
-        linear_row = psum.tile([1, C], F32, name="linear_row")
-        field_cols_ps = psum.tile([BLOCK, BLOCKS], F32, name="field_cols_ps")
-        nc.tensor.matmul(
-            field_cols_ps[:], field_rows[:], identity[0:BLOCKS, 0:BLOCKS], start=True, stop=True
+        weight_cols_ps = psum.tile([BLOCK, WEIGHT_BLOCKS], F32, name="weight_cols_ps")
+        nc.tensor.transpose(
+            weight_cols_ps[:], weight_rows[:], identity[0:WEIGHT_BLOCKS, 0:WEIGHT_BLOCKS]
         )
-        field_cols = held.tile([BLOCK, BLOCKS], F32, name="field_cols")
-        nc.scalar.activation(field_cols[:], field_cols_ps[:], IDENTITY)
+        weight_cols = held.tile([BLOCK, WEIGHT_BLOCKS], F32, name="weight_cols")
+        nc.scalar.activation(weight_cols[:], weight_cols_ps[:], IDENTITY)
 
-        for g in range(BLOCKS // BLOCKS_IN_BANK):
-            flipped_ps = banks.tile([BLOCK, BANK], F32, name="flipped_ps")
-            for i in range(BLOCKS_IN_BANK):
-                b = g * BLOCKS_IN_BANK + i
-                nc.tensor.transpose(
-                    flipped_ps[:, i * BLOCK : (i + 1) * BLOCK],
-                    table[:, b * BLOCK : (b + 1) * BLOCK],
-                    identity[:],
-                )
-            flipped = stream.tile([BLOCK, BANK], F32, name="flipped")
-            nc.scalar.activation(flipped[:], flipped_ps[:], IDENTITY)
-            for i in range(BLOCKS_IN_BANK):
-                b = g * BLOCKS_IN_BANK + i
-                nc.tensor.matmul(
-                    linear_row[:],
-                    field_cols[:, b : b + 1],
-                    flipped[:, i * BLOCK : (i + 1) * BLOCK],
-                    start=(b == 0),
-                    stop=(b == BLOCKS - 1),
-                )
-        linear_and_bias = held.tile([1, C], F32, name="linear_and_bias")
-        nc.scalar.activation(linear_and_bias[:], linear_row[:], IDENTITY, bias=bias_one[:, 0:1])
+        energy_row = psum.tile([1, C], F32, name="energy_row")
+
+        def add_weighted_columns(values, first_weight):
+            for g in range(values.shape[1] // BANK):
+                flipped_ps = banks.tile([BLOCK, BANK], F32, name="flipped_ps")
+                for i in range(BLOCKS_IN_BANK):
+                    b = g * BLOCKS_IN_BANK + i
+                    nc.tensor.transpose(
+                        flipped_ps[:, i * BLOCK : (i + 1) * BLOCK],
+                        values[:, b * BLOCK : (b + 1) * BLOCK],
+                        identity[:],
+                    )
+                flipped = stream.tile([BLOCK, BANK], F32, name="flipped")
+                nc.scalar.activation(flipped[:], flipped_ps[:], IDENTITY)
+                for i in range(BLOCKS_IN_BANK):
+                    w = first_weight + g * BLOCKS_IN_BANK + i
+                    nc.tensor.matmul(
+                        energy_row[:],
+                        weight_cols[:, w : w + 1],
+                        flipped[:, i * BLOCK : (i + 1) * BLOCK],
+                        start=(w == 0),
+                        stop=False,
+                    )
+
+        add_weighted_columns(table[:], 0)
 
         sums = held.tile([C, PIECES], F32, name="sums")
-        pair_row = psum.tile([1, C], F32, name="pair_row")
         for p in range(PIECES):
             pairs = slice(p * PIECE, (p + 1) * PIECE)
             first = (p * PIECE) % S
-            partner = stream.tile([C, PIECE], F32, name="partner")
-            nc.gpsimd.tensor_tensor(
-                partner[:], table[:, first : first + PIECE], coup_all[:, pairs], MULT
-            )
             picked = table[:].indirect(offsets[:, p * (PIECE // 16) : (p + 1) * (PIECE // 16)])
-            pairwise = stream.tile([C, PIECE], F32, name="pairwise")
-            nc.vector.tensor_tensor(pairwise[:], picked, partner[:], MULT)
-            spent = stream.tile([C, PIECE], F32, name="spent")
-            nc.scalar.activation(spent[:], pairwise[:], IDENTITY, accum_out=sums[:, p : p + 1])
-            nc.tensor.matmul(
-                pair_row[:], sums[:, p : p + 1], identity[:], start=(p == 0), stop=(p == PIECES - 1)
-            )
+            products = product_pool.tile([C, PIECE], F32, name="products")
+            nc.vector.tensor_tensor(products[:], picked, partners[:, first : first + PIECE], MULT)
+            if p < TENSOR_PIECES:
+                add_weighted_columns(products[:], FIELD_BLOCKS + p * PIECE_BLOCKS)
+            else:
+                weighted = stream.tile([C, PIECE], F32, name="weighted")
+                nc.vector.scalar_tensor_tensor(
+                    weighted[:],
+                    products[:],
+                    1.0,
+                    coup_all[:, pairs],
+                    MULT,
+                    MULT,
+                    accum_out=sums[:, p : p + 1],
+                )
+                nc.tensor.matmul(
+                    energy_row[:], sums[:, p : p + 1], identity[:], start=False, stop=(p == PIECES - 1)
+                )
 
         energy = held.tile([1, C], F32, name="energy")
-        nc.vector.tensor_tensor(energy[:], pair_row[:], linear_and_bias[:], ADD)
+        nc.vector.tensor_scalar_add(energy[:], energy_row[:], bias_one[:, 0:1])
         nc.sync.dma_start(out.rearrange("c o -> o c"), energy[:])

@@ -9,14 +9,15 @@ IDENTITY = mybir.ActivationFunctionType.Identity
 C = 128
 S = 4096
 N = 8192
-PIECE = 1024
+PIECE = 2048
 PIECES = N // PIECE
+CHUNK = 1024
 BLOCK = 128
 BANK = 512
 BLOCKS_IN_BANK = BANK // BLOCK
 FIELD_BLOCKS = S // BLOCK
 PIECE_BLOCKS = PIECE // BLOCK
-TENSOR_PIECES = 2
+TENSOR_PIECES = 1
 WEIGHT_BLOCKS = FIELD_BLOCKS + TENSOR_PIECES * PIECE_BLOCKS
 
 FLOPS = C * (2 * S + 3 * N)
@@ -28,24 +29,24 @@ def tile_linearpairwisemodule_kernel(tc, x, field, coup, bias, offs, out):
     coup_blocks = coup.rearrange("o (b s) -> (o b) s", s=BLOCK)
     with (
         tc.tile_pool(name="held", bufs=1) as held,
-        tc.tile_pool(name="stream", bufs=3) as stream,
-        tc.tile_pool(name="product_pool", bufs=TENSOR_PIECES + 3) as product_pool,
+        tc.tile_pool(name="stream", bufs=4) as stream,
+        tc.tile_pool(name="product_pool", bufs=TENSOR_PIECES + 2) as product_pool,
         tc.psum_pool(name="psum", bufs=1) as psum,
-        tc.psum_pool(name="banks", bufs=2) as banks,
+        tc.psum_pool(name="banks", bufs=4) as banks,
     ):
         weight_rows = held.tile([WEIGHT_BLOCKS, BLOCK], F32, name="weight_rows")
-        nc.sync.dma_start(
+        nc.scalar.dma_start(
             weight_rows[0:FIELD_BLOCKS, :], field.rearrange("o (b s) -> (o b) s", s=BLOCK)
         )
-        nc.sync.dma_start(
+        nc.scalar.dma_start(
             weight_rows[FIELD_BLOCKS:WEIGHT_BLOCKS, :], coup_blocks[0 : TENSOR_PIECES * PIECE_BLOCKS, :]
         )
         bias_one = held.tile([1, 1], F32, name="bias_one")
-        nc.sync.dma_start(bias_one[:], bias.unsqueeze(0))
+        nc.scalar.dma_start(bias_one[:], bias.unsqueeze(0))
 
         table = held.tile([C, S], F32, name="table")
-        for p in range(S // PIECE):
-            cols = slice(p * PIECE, (p + 1) * PIECE)
+        for k in range(S // CHUNK):
+            cols = slice(k * CHUNK, (k + 1) * CHUNK)
             nc.sync.dma_start(table[:, cols], x[:, cols])
         offsets = held.tile([C, N // 16], U16, name="offsets")
         nc.sync.dma_start(offsets[:], offs)
@@ -55,8 +56,8 @@ def tile_linearpairwisemodule_kernel(tc, x, field, coup, bias, offs, out):
             nc.sync.dma_start(coup_all[:, cols], coup_row[cols].partition_broadcast(C))
 
         partners = held.tile([C, S], F32, name="partners")
-        for p in range(S // PIECE):
-            cols = slice(p * PIECE, (p + 1) * PIECE)
+        for k in range(S // CHUNK):
+            cols = slice(k * CHUNK, (k + 1) * CHUNK)
             nc.scalar.activation(partners[:, cols], table[:, cols], IDENTITY)
 
         identity = held.tile([C, C], F32, name="identity")

@@ -9,15 +9,14 @@ IDENTITY = mybir.ActivationFunctionType.Identity
 C = 128
 S = 4096
 N = 8192
-PIECE = 2048
+PIECE = 1024
 PIECES = N // PIECE
-CHUNK = 1024
 BLOCK = 128
 BANK = 512
 BLOCKS_IN_BANK = BANK // BLOCK
 FIELD_BLOCKS = S // BLOCK
 PIECE_BLOCKS = PIECE // BLOCK
-TENSOR_PIECES = 1
+TENSOR_PIECES = 2
 WEIGHT_BLOCKS = FIELD_BLOCKS + TENSOR_PIECES * PIECE_BLOCKS
 
 FLOPS = C * (2 * S + 3 * N)
@@ -30,7 +29,7 @@ def tile_linearpairwisemodule_kernel(tc, x, field, coup, bias, offs, out):
     with (
         tc.tile_pool(name="held", bufs=1) as held,
         tc.tile_pool(name="stream", bufs=4) as stream,
-        tc.tile_pool(name="product_pool", bufs=TENSOR_PIECES + 2) as product_pool,
+        tc.tile_pool(name="product_pool", bufs=TENSOR_PIECES + 3) as product_pool,
         tc.psum_pool(name="psum", bufs=1) as psum,
         tc.psum_pool(name="banks", bufs=4) as banks,
     ):
@@ -45,8 +44,8 @@ def tile_linearpairwisemodule_kernel(tc, x, field, coup, bias, offs, out):
         nc.scalar.dma_start(bias_one[:], bias.unsqueeze(0))
 
         table = held.tile([C, S], F32, name="table")
-        for k in range(S // CHUNK):
-            cols = slice(k * CHUNK, (k + 1) * CHUNK)
+        for p in range(S // PIECE):
+            cols = slice(p * PIECE, (p + 1) * PIECE)
             nc.sync.dma_start(table[:, cols], x[:, cols])
         offsets = held.tile([C, N // 16], U16, name="offsets")
         nc.sync.dma_start(offsets[:], offs)
@@ -56,8 +55,8 @@ def tile_linearpairwisemodule_kernel(tc, x, field, coup, bias, offs, out):
             nc.sync.dma_start(coup_all[:, cols], coup_row[cols].partition_broadcast(C))
 
         partners = held.tile([C, S], F32, name="partners")
-        for k in range(S // CHUNK):
-            cols = slice(k * CHUNK, (k + 1) * CHUNK)
+        for p in range(S // PIECE):
+            cols = slice(p * PIECE, (p + 1) * PIECE)
             nc.scalar.activation(partners[:, cols], table[:, cols], IDENTITY)
 
         identity = held.tile([C, C], F32, name="identity")

@@ -9,15 +9,16 @@ IDENTITY = mybir.ActivationFunctionType.Identity
 C = 128
 S = 4096
 N = 8192
-PIECE = 1024
-PIECES = N // PIECE
+CHUNK = 1024
 BLOCK = 128
 BANK = 512
 BLOCKS_IN_BANK = BANK // BLOCK
 FIELD_BLOCKS = S // BLOCK
-PIECE_BLOCKS = PIECE // BLOCK
-TENSOR_PIECES = 2
-WEIGHT_BLOCKS = FIELD_BLOCKS + TENSOR_PIECES * PIECE_BLOCKS
+TENSOR_PAIRS = 3072
+COUP_BLOCKS = S // BLOCK
+WEIGHT_BLOCKS = FIELD_BLOCKS + COUP_BLOCKS
+CUTS = (0, TENSOR_PAIRS, S, S + S // 2, N)
+PIECES = len(CUTS) - 1
 
 FLOPS = C * (2 * S + 3 * N)
 
@@ -29,34 +30,32 @@ def tile_linearpairwisemodule_kernel(tc, x, field, coup, bias, offs, out):
     with (
         tc.tile_pool(name="held", bufs=1) as held,
         tc.tile_pool(name="stream", bufs=4) as stream,
-        tc.tile_pool(name="product_pool", bufs=TENSOR_PIECES + 3) as product_pool,
+        tc.tile_pool(name="product_pool", bufs=3) as product_pool,
         tc.psum_pool(name="psum", bufs=1) as psum,
         tc.psum_pool(name="banks", bufs=4) as banks,
     ):
         weight_rows = held.tile([WEIGHT_BLOCKS, BLOCK], F32, name="weight_rows")
-        nc.scalar.dma_start(
+        nc.sync.dma_start(
             weight_rows[0:FIELD_BLOCKS, :], field.rearrange("o (b s) -> (o b) s", s=BLOCK)
         )
-        nc.scalar.dma_start(
-            weight_rows[FIELD_BLOCKS:WEIGHT_BLOCKS, :], coup_blocks[0 : TENSOR_PIECES * PIECE_BLOCKS, :]
-        )
+        nc.sync.dma_start(weight_rows[FIELD_BLOCKS:WEIGHT_BLOCKS, :], coup_blocks[0:COUP_BLOCKS, :])
         bias_one = held.tile([1, 1], F32, name="bias_one")
-        nc.scalar.dma_start(bias_one[:], bias.unsqueeze(0))
+        nc.sync.dma_start(bias_one[:], bias.unsqueeze(0))
 
         table = held.tile([C, S], F32, name="table")
-        for p in range(S // PIECE):
-            cols = slice(p * PIECE, (p + 1) * PIECE)
+        for k in range(S // CHUNK):
+            cols = slice(k * CHUNK, (k + 1) * CHUNK)
             nc.sync.dma_start(table[:, cols], x[:, cols])
         offsets = held.tile([C, N // 16], U16, name="offsets")
         nc.sync.dma_start(offsets[:], offs)
         coup_all = held.tile([C, N], F32, name="coup_all")
-        for p in range(TENSOR_PIECES, PIECES):
-            cols = slice(p * PIECE, (p + 1) * PIECE)
+        for k in range(TENSOR_PAIRS // CHUNK, N // CHUNK):
+            cols = slice(k * CHUNK, (k + 1) * CHUNK)
             nc.sync.dma_start(coup_all[:, cols], coup_row[cols].partition_broadcast(C))
 
         partners = held.tile([C, S], F32, name="partners")
-        for p in range(S // PIECE):
-            cols = slice(p * PIECE, (p + 1) * PIECE)
+        for k in range(S // CHUNK):
+            cols = slice(k * CHUNK, (k + 1) * CHUNK)
             nc.scalar.activation(partners[:, cols], table[:, cols], IDENTITY)
 
         identity = held.tile([C, C], F32, name="identity")
@@ -97,15 +96,16 @@ def tile_linearpairwisemodule_kernel(tc, x, field, coup, bias, offs, out):
 
         sums = held.tile([C, PIECES], F32, name="sums")
         for p in range(PIECES):
-            pairs = slice(p * PIECE, (p + 1) * PIECE)
-            first = (p * PIECE) % S
-            picked = table[:].indirect(offsets[:, p * (PIECE // 16) : (p + 1) * (PIECE // 16)])
-            products = product_pool.tile([C, PIECE], F32, name="products")
-            nc.vector.tensor_tensor(products[:], picked, partners[:, first : first + PIECE], MULT)
-            if p < TENSOR_PIECES:
-                add_weighted_columns(products[:], FIELD_BLOCKS + p * PIECE_BLOCKS)
+            pairs = slice(CUTS[p], CUTS[p + 1])
+            width = CUTS[p + 1] - CUTS[p]
+            first = CUTS[p] % S
+            picked = table[:].indirect(offsets[:, CUTS[p] // 16 : CUTS[p + 1] // 16])
+            products = product_pool.tile([C, width], F32, name="products")
+            nc.vector.tensor_tensor(products[:], picked, partners[:, first : first + width], MULT)
+            if CUTS[p + 1] <= TENSOR_PAIRS:
+                add_weighted_columns(products[:], FIELD_BLOCKS)
             else:
-                weighted = stream.tile([C, PIECE], F32, name="weighted")
+                weighted = stream.tile([C, width], F32, name="weighted")
                 nc.vector.scalar_tensor_tensor(
                     weighted[:],
                     products[:],

@@ -12,33 +12,33 @@ N = 8192
 CHUNK = 1024
 BLOCK = 128
 BANK = 512
-BLOCKS_IN_BANK = BANK // BLOCK
+QUARTERS = BANK // BLOCK
+QUARTER_ROWS = C // QUARTERS
 FIELD_BLOCKS = S // BLOCK
-TENSOR_PAIRS = 3072
-COUP_BLOCKS = S // BLOCK
+COUP_BLOCKS = N // BLOCK
 WEIGHT_BLOCKS = FIELD_BLOCKS + COUP_BLOCKS
-CUTS = (0, TENSOR_PAIRS, S, S + S // 2, N)
-PIECES = len(CUTS) - 1
+PIECE = 1024
+LAG = 2
 
 FLOPS = C * (2 * S + 3 * N)
 
 
 def tile_linearpairwisemodule_kernel(tc, x, field, coup, bias, offs, out):
     nc = tc.nc
-    coup_row = coup.rearrange("o n -> (o n)")
-    coup_blocks = coup.rearrange("o (b s) -> (o b) s", s=BLOCK)
     with (
         tc.tile_pool(name="held", bufs=1) as held,
-        tc.tile_pool(name="stream", bufs=4) as stream,
-        tc.tile_pool(name="product_pool", bufs=3) as product_pool,
+        tc.tile_pool(name="stream", bufs=LAG + 2) as stream,
         tc.psum_pool(name="psum", bufs=1) as psum,
-        tc.psum_pool(name="banks", bufs=4) as banks,
+        tc.psum_pool(name="banks", bufs=LAG + 2) as banks,
     ):
-        weight_rows = held.tile([WEIGHT_BLOCKS, BLOCK], F32, name="weight_rows")
+        weight_rows = held.tile([C, BLOCK], F32, name="weight_rows")
+        nc.vector.memset(weight_rows[WEIGHT_BLOCKS:C, :], 0.0)
         nc.sync.dma_start(
             weight_rows[0:FIELD_BLOCKS, :], field.rearrange("o (b s) -> (o b) s", s=BLOCK)
         )
-        nc.sync.dma_start(weight_rows[FIELD_BLOCKS:WEIGHT_BLOCKS, :], coup_blocks[0:COUP_BLOCKS, :])
+        nc.sync.dma_start(
+            weight_rows[FIELD_BLOCKS:WEIGHT_BLOCKS, :], coup.rearrange("o (b s) -> (o b) s", s=BLOCK)
+        )
         bias_one = held.tile([1, 1], F32, name="bias_one")
         nc.sync.dma_start(bias_one[:], bias.unsqueeze(0))
 
@@ -48,77 +48,78 @@ def tile_linearpairwisemodule_kernel(tc, x, field, coup, bias, offs, out):
             nc.sync.dma_start(table[:, cols], x[:, cols])
         offsets = held.tile([C, N // 16], U16, name="offsets")
         nc.sync.dma_start(offsets[:], offs)
-        coup_all = held.tile([C, N], F32, name="coup_all")
-        for k in range(TENSOR_PAIRS // CHUNK, N // CHUNK):
-            cols = slice(k * CHUNK, (k + 1) * CHUNK)
-            nc.sync.dma_start(coup_all[:, cols], coup_row[cols].partition_broadcast(C))
-
-        partners = held.tile([C, S], F32, name="partners")
-        for k in range(S // CHUNK):
-            cols = slice(k * CHUNK, (k + 1) * CHUNK)
-            nc.scalar.activation(partners[:, cols], table[:, cols], IDENTITY)
 
         identity = held.tile([C, C], F32, name="identity")
         make_identity(nc, identity[:])
+        zeros = held.tile([C, C], F32, name="zeros")
+        nc.vector.memset(zeros[:], 0.0)
+        ones = held.tile([C, 1], F32, name="ones")
+        nc.vector.memset(ones[:], 1.0)
 
-        weight_cols_ps = psum.tile([BLOCK, WEIGHT_BLOCKS], F32, name="weight_cols_ps")
-        nc.tensor.transpose(
-            weight_cols_ps[:], weight_rows[:], identity[0:WEIGHT_BLOCKS, 0:WEIGHT_BLOCKS]
-        )
-        weight_cols = held.tile([BLOCK, WEIGHT_BLOCKS], F32, name="weight_cols")
+        weight_cols_ps = psum.tile([BLOCK, C], F32, name="weight_cols_ps")
+        nc.tensor.transpose(weight_cols_ps[:], weight_rows[:], identity[:])
+        weight_cols = held.tile([BLOCK, C], F32, name="weight_cols")
         nc.scalar.activation(weight_cols[:], weight_cols_ps[:], IDENTITY)
 
-        energy_row = psum.tile([1, C], F32, name="energy_row")
+        partial = psum.tile([C, C], F32, name="partial")
+        nc.tensor.matmul(partial[:], zeros[:], identity[:], start=True, stop=False)
+
+        waiting = []
+
+        def weigh_oldest():
+            flipped, first_weight = waiting[0]
+            waiting.remove(waiting[0])
+            for q in range(QUARTERS):
+                w = first_weight + q
+                nc.tensor.matmul(
+                    partial[q * QUARTER_ROWS : q * QUARTER_ROWS + 1, :],
+                    weight_cols[:, w : w + 1],
+                    flipped[:, q * BLOCK : (q + 1) * BLOCK],
+                    start=False,
+                    stop=(w >= WEIGHT_BLOCKS - QUARTERS),
+                )
 
         def add_weighted_columns(values, first_weight):
             for g in range(values.shape[1] // BANK):
                 flipped_ps = banks.tile([BLOCK, BANK], F32, name="flipped_ps")
-                for i in range(BLOCKS_IN_BANK):
-                    b = g * BLOCKS_IN_BANK + i
+                for q in range(QUARTERS):
+                    b = g * QUARTERS + q
                     nc.tensor.transpose(
-                        flipped_ps[:, i * BLOCK : (i + 1) * BLOCK],
+                        flipped_ps[:, q * BLOCK : (q + 1) * BLOCK],
                         values[:, b * BLOCK : (b + 1) * BLOCK],
                         identity[:],
                     )
                 flipped = stream.tile([BLOCK, BANK], F32, name="flipped")
                 nc.scalar.activation(flipped[:], flipped_ps[:], IDENTITY)
-                for i in range(BLOCKS_IN_BANK):
-                    w = first_weight + g * BLOCKS_IN_BANK + i
-                    nc.tensor.matmul(
-                        energy_row[:],
-                        weight_cols[:, w : w + 1],
-                        flipped[:, i * BLOCK : (i + 1) * BLOCK],
-                        start=(w == 0),
-                        stop=False,
-                    )
+                waiting.append((flipped, first_weight + g * QUARTERS))
+                if len(waiting) > LAG:
+                    weigh_oldest()
 
-        add_weighted_columns(table[:], 0)
-
-        sums = held.tile([C, PIECES], F32, name="sums")
-        for p in range(PIECES):
-            pairs = slice(CUTS[p], CUTS[p + 1])
-            width = CUTS[p + 1] - CUTS[p]
-            first = CUTS[p] % S
-            picked = table[:].indirect(offsets[:, CUTS[p] // 16 : CUTS[p + 1] // 16])
-            products = product_pool.tile([C, width], F32, name="products")
-            nc.vector.tensor_tensor(products[:], picked, partners[:, first : first + width], MULT)
-            if CUTS[p + 1] <= TENSOR_PAIRS:
-                add_weighted_columns(products[:], FIELD_BLOCKS)
+        partners = held.tile([C, S], F32, name="partners")
+        for k in range(S // CHUNK):
+            cols = slice(k * CHUNK, (k + 1) * CHUNK)
+            if k < S // CHUNK - 1:
+                nc.vector.tensor_copy(partners[:, cols], table[:, cols])
             else:
-                weighted = stream.tile([C, width], F32, name="weighted")
-                nc.vector.scalar_tensor_tensor(
-                    weighted[:],
-                    products[:],
-                    1.0,
-                    coup_all[:, pairs],
-                    MULT,
-                    MULT,
-                    accum_out=sums[:, p : p + 1],
-                )
-                nc.tensor.matmul(
-                    energy_row[:], sums[:, p : p + 1], identity[:], start=False, stop=(p == PIECES - 1)
-                )
+                nc.scalar.activation(partners[:, cols], table[:, cols], IDENTITY)
+            add_weighted_columns(table[:, cols], k * CHUNK // BLOCK)
 
+        products = held.tile([C, N], F32, name="products")
+        for p in range(N // PIECE):
+            pairs = slice(p * PIECE, (p + 1) * PIECE)
+            first = p * PIECE % S
+            picked = table[:].indirect(offsets[:, p * PIECE // 16 : (p + 1) * PIECE // 16])
+            nc.vector.tensor_tensor(
+                products[:, pairs], picked, partners[:, first : first + PIECE], MULT
+            )
+            add_weighted_columns(products[:, pairs], FIELD_BLOCKS + p * PIECE // BLOCK)
+        for u in range(LAG):
+            weigh_oldest()
+
+        partial_sb = held.tile([C, C], F32, name="partial_sb")
+        nc.vector.tensor_copy(partial_sb[:], partial[:])
+        energy_row = psum.tile([1, C], F32, name="energy_row")
+        nc.tensor.matmul(energy_row[:], ones[:], partial_sb[:], start=True, stop=True)
         energy = held.tile([1, C], F32, name="energy")
         nc.vector.tensor_scalar_add(energy[:], energy_row[:], bias_one[:, 0:1])
         nc.sync.dma_start(out.rearrange("c o -> o c"), energy[:])

@@ -18,7 +18,10 @@ FIELD_BLOCKS = S // BLOCK
 COUP_BLOCKS = N // BLOCK
 WEIGHT_BLOCKS = FIELD_BLOCKS + COUP_BLOCKS
 PIECE = 1024
-LAG = 2
+UNITS_IN_ROUND = CHUNK // BANK
+assert PIECE == CHUNK
+VECTOR_PAIRS = PIECE
+TENSOR_BLOCKS = FIELD_BLOCKS + (N - VECTOR_PAIRS) // BLOCK
 
 FLOPS = C * (2 * S + 3 * N)
 
@@ -27,9 +30,9 @@ def tile_linearpairwisemodule_kernel(tc, x, field, coup, bias, offs, out):
     nc = tc.nc
     with (
         tc.tile_pool(name="held", bufs=1) as held,
-        tc.tile_pool(name="stream", bufs=LAG + 2) as stream,
+        tc.tile_pool(name="stream", bufs=2 * UNITS_IN_ROUND + 1) as stream,
         tc.psum_pool(name="psum", bufs=1) as psum,
-        tc.psum_pool(name="banks", bufs=LAG + 2) as banks,
+        tc.psum_pool(name="banks", bufs=2 * UNITS_IN_ROUND) as banks,
     ):
         weight_rows = held.tile([C, BLOCK], F32, name="weight_rows")
         nc.vector.memset(weight_rows[WEIGHT_BLOCKS:C, :], 0.0)
@@ -48,6 +51,10 @@ def tile_linearpairwisemodule_kernel(tc, x, field, coup, bias, offs, out):
             nc.sync.dma_start(table[:, cols], x[:, cols])
         offsets = held.tile([C, N // 16], U16, name="offsets")
         nc.sync.dma_start(offsets[:], offs)
+        coup_vector = held.tile([C, VECTOR_PAIRS], F32, name="coup_vector")
+        nc.sync.dma_start(
+            coup_vector[:], coup.rearrange("o n -> (o n)")[N - VECTOR_PAIRS : N].partition_broadcast(C)
+        )
 
         identity = held.tile([C, C], F32, name="identity")
         make_identity(nc, identity[:])
@@ -66,20 +73,21 @@ def tile_linearpairwisemodule_kernel(tc, x, field, coup, bias, offs, out):
 
         waiting = []
 
-        def weigh_oldest():
-            flipped, first_weight = waiting[0]
-            waiting.remove(waiting[0])
-            for q in range(QUARTERS):
-                w = first_weight + q
-                nc.tensor.matmul(
-                    partial[q * QUARTER_ROWS : q * QUARTER_ROWS + 1, :],
-                    weight_cols[:, w : w + 1],
-                    flipped[:, q * BLOCK : (q + 1) * BLOCK],
-                    start=False,
-                    stop=(w >= WEIGHT_BLOCKS - QUARTERS),
-                )
+        def weigh_waiting_round():
+            for flipped, first_weight in waiting:
+                for q in range(QUARTERS):
+                    w = first_weight + q
+                    nc.tensor.matmul(
+                        partial[q * QUARTER_ROWS : q * QUARTER_ROWS + 1, :],
+                        weight_cols[:, w : w + 1],
+                        flipped[:, q * BLOCK : (q + 1) * BLOCK],
+                        start=False,
+                        stop=(w >= TENSOR_BLOCKS - QUARTERS),
+                    )
+            waiting.clear()
 
         def add_weighted_columns(values, first_weight):
+            flipped_round = []
             for g in range(values.shape[1] // BANK):
                 flipped_ps = banks.tile([BLOCK, BANK], F32, name="flipped_ps")
                 for q in range(QUARTERS):
@@ -91,9 +99,9 @@ def tile_linearpairwisemodule_kernel(tc, x, field, coup, bias, offs, out):
                     )
                 flipped = stream.tile([BLOCK, BANK], F32, name="flipped")
                 nc.scalar.activation(flipped[:], flipped_ps[:], IDENTITY)
-                waiting.append((flipped, first_weight + g * QUARTERS))
-                if len(waiting) > LAG:
-                    weigh_oldest()
+                flipped_round.append((flipped, first_weight + g * QUARTERS))
+            weigh_waiting_round()
+            waiting.extend(flipped_round)
 
         partners = held.tile([C, S], F32, name="partners")
         for k in range(S // CHUNK):
@@ -112,14 +120,26 @@ def tile_linearpairwisemodule_kernel(tc, x, field, coup, bias, offs, out):
             nc.vector.tensor_tensor(
                 products[:, pairs], picked, partners[:, first : first + PIECE], MULT
             )
-            add_weighted_columns(products[:, pairs], FIELD_BLOCKS + p * PIECE // BLOCK)
-        for u in range(LAG):
-            weigh_oldest()
+            if (p + 1) * PIECE <= N - VECTOR_PAIRS:
+                add_weighted_columns(products[:, pairs], FIELD_BLOCKS + p * PIECE // BLOCK)
+        weigh_waiting_round()
+        weighted = held.tile([C, VECTOR_PAIRS], F32, name="weighted")
+        vector_sum = held.tile([C, 1], F32, name="vector_sum")
+        nc.vector.scalar_tensor_tensor(
+            weighted[:],
+            products[:, N - VECTOR_PAIRS : N],
+            1.0,
+            coup_vector[:],
+            MULT,
+            MULT,
+            accum_out=vector_sum[:],
+        )
 
         partial_sb = held.tile([C, C], F32, name="partial_sb")
-        nc.vector.tensor_copy(partial_sb[:], partial[:])
+        nc.scalar.activation(partial_sb[:], partial[:], IDENTITY)
         energy_row = psum.tile([1, C], F32, name="energy_row")
-        nc.tensor.matmul(energy_row[:], ones[:], partial_sb[:], start=True, stop=True)
+        nc.tensor.matmul(energy_row[:], ones[:], partial_sb[:], start=True, stop=False)
+        nc.tensor.matmul(energy_row[:], vector_sum[:], identity[:], start=False, stop=True)
         energy = held.tile([1, C], F32, name="energy")
         nc.vector.tensor_scalar_add(energy[:], energy_row[:], bias_one[:, 0:1])
         nc.sync.dma_start(out.rearrange("c o -> o c"), energy[:])

@@ -34,17 +34,6 @@ def tile_linearpairwisemodule_kernel(tc, x, field, coup, bias, offs, out):
         tc.psum_pool(name="psum", bufs=1) as psum,
         tc.psum_pool(name="banks", bufs=2 * UNITS_IN_ROUND) as banks,
     ):
-        weight_rows = held.tile([C, BLOCK], F32, name="weight_rows")
-        nc.vector.memset(weight_rows[WEIGHT_BLOCKS:C, :], 0.0)
-        nc.sync.dma_start(
-            weight_rows[0:FIELD_BLOCKS, :], field.rearrange("o (b s) -> (o b) s", s=BLOCK)
-        )
-        nc.sync.dma_start(
-            weight_rows[FIELD_BLOCKS:WEIGHT_BLOCKS, :], coup.rearrange("o (b s) -> (o b) s", s=BLOCK)
-        )
-        bias_one = held.tile([1, 1], F32, name="bias_one")
-        nc.sync.dma_start(bias_one[:], bias.unsqueeze(0))
-
         table = held.tile([C, S], F32, name="table")
         for k in range(S // CHUNK):
             cols = slice(k * CHUNK, (k + 1) * CHUNK)
@@ -55,6 +44,17 @@ def tile_linearpairwisemodule_kernel(tc, x, field, coup, bias, offs, out):
         nc.sync.dma_start(
             coup_vector[:], coup.rearrange("o n -> (o n)")[N - VECTOR_PAIRS : N].partition_broadcast(C)
         )
+
+        weight_rows = held.tile([C, BLOCK], F32, name="weight_rows")
+        nc.vector.memset(weight_rows[WEIGHT_BLOCKS:C, :], 0.0)
+        nc.scalar.dma_start(
+            weight_rows[0:FIELD_BLOCKS, :], field.rearrange("o (b s) -> (o b) s", s=BLOCK)
+        )
+        nc.scalar.dma_start(
+            weight_rows[FIELD_BLOCKS:WEIGHT_BLOCKS, :], coup.rearrange("o (b s) -> (o b) s", s=BLOCK)
+        )
+        bias_one = held.tile([1, 1], F32, name="bias_one")
+        nc.scalar.dma_start(bias_one[:], bias.unsqueeze(0))
 
         identity = held.tile([C, C], F32, name="identity")
         make_identity(nc, identity[:])

@@ -9,6 +9,7 @@ IDENTITY = mybir.ActivationFunctionType.Identity
 C = 128
 S = 4096
 N = 8192
+LOAD = 2048
 CHUNK = 1024
 BLOCK = 128
 BANK = 512
@@ -35,8 +36,8 @@ def tile_linearpairwisemodule_kernel(tc, x, field, coup, bias, offs, out):
         tc.psum_pool(name="banks", bufs=2 * UNITS_IN_ROUND) as banks,
     ):
         table = held.tile([C, S], F32, name="table")
-        for k in range(S // CHUNK):
-            cols = slice(k * CHUNK, (k + 1) * CHUNK)
+        for k in range(S // LOAD):
+            cols = slice(k * LOAD, (k + 1) * LOAD)
             nc.sync.dma_start(table[:, cols], x[:, cols])
         offsets = held.tile([C, N // 16], U16, name="offsets")
         nc.sync.dma_start(offsets[:], offs)

@@ -107,7 +107,7 @@ def tile_linearpairwisemodule_kernel(tc, x, field, coup, bias, offs, out):
         partners = held.tile([C, S], F32, name="partners")
         for k in range(S // CHUNK):
             cols = slice(k * CHUNK, (k + 1) * CHUNK)
-            if k < S // CHUNK - 1:
+            if (k + 1) * CHUNK <= S - LOAD:
                 nc.vector.tensor_copy(partners[:, cols], table[:, cols])
             else:
                 nc.scalar.activation(partners[:, cols], table[:, cols], IDENTITY)
@@ -140,7 +140,9 @@ def tile_linearpairwisemodule_kernel(tc, x, field, coup, bias, offs, out):
         nc.scalar.activation(partial_sb[:], partial[:], IDENTITY)
         energy_row = psum.tile([1, C], F32, name="energy_row")
         nc.tensor.matmul(energy_row[:], ones[:], partial_sb[:], start=True, stop=False)
-        nc.tensor.matmul(energy_row[:], vector_sum[:], identity[:], start=False, stop=True)
+        nc.tensor.matmul(
+            energy_row[:], vector_sum[:], identity[:], start=False, stop=True, is_transpose=True
+        )
         energy = held.tile([1, C], F32, name="energy")
         nc.vector.tensor_scalar_add(energy[:], energy_row[:], bias_one[:, 0:1])
         nc.sync.dma_start(out.rearrange("c o -> o c"), energy[:])

@@ -1,10 +1,12 @@
 import concourse.mybir as mybir
-from concourse.masks import make_identity
 
 F32 = mybir.dt.float32
 U16 = mybir.dt.uint16
 MULT = mybir.AluOpType.mult
+ADD = mybir.AluOpType.add
+IS_EQUAL = mybir.AluOpType.is_equal
 IDENTITY = mybir.ActivationFunctionType.Identity
+AXIS_X = mybir.AxisListType.X
 
 C = 128
 S = 4096
@@ -15,14 +17,15 @@ BLOCK = 128
 BANK = 512
 QUARTERS = BANK // BLOCK
 QUARTER_ROWS = C // QUARTERS
+SQUARE = 32
 FIELD_BLOCKS = S // BLOCK
 COUP_BLOCKS = N // BLOCK
 WEIGHT_BLOCKS = FIELD_BLOCKS + COUP_BLOCKS
-PIECE = 1024
-UNITS_IN_ROUND = CHUNK // BANK
-assert PIECE == CHUNK
-VECTOR_PAIRS = PIECE
-TENSOR_BLOCKS = FIELD_BLOCKS + (N - VECTOR_PAIRS) // BLOCK
+
+WEIGHTED_UNITS = (0, BANK, S)
+EARLIER, LATEST = CHUNK, BANK
+PLAIN = [(k + c, CHUNK) for c in range(CHUNK, S, CHUNK) for k in range(0, N, S)] + [(S + BANK, BANK)]
+PLAIN_PAIRS = N - EARLIER - LATEST
 
 FLOPS = C * (2 * S + 3 * N)
 
@@ -31,64 +34,91 @@ def tile_linearpairwisemodule_kernel(tc, x, field, coup, bias, offs, out):
     nc = tc.nc
     with (
         tc.tile_pool(name="held", bufs=1) as held,
-        tc.tile_pool(name="stream", bufs=2 * UNITS_IN_ROUND + 1) as stream,
+        tc.tile_pool(name="stream", bufs=3) as stream,
         tc.psum_pool(name="psum", bufs=1) as psum,
-        tc.psum_pool(name="banks", bufs=2 * UNITS_IN_ROUND) as banks,
+        tc.psum_pool(name="banks", bufs=2 * CHUNK // BANK) as banks,
     ):
+        weight_rows = held.tile([C, BLOCK], F32, name="weight_rows")
+        nc.vector.memset(weight_rows[WEIGHT_BLOCKS:C, :], 0.0)
+        nc.sync.dma_start(
+            weight_rows[FIELD_BLOCKS:WEIGHT_BLOCKS, :], coup.rearrange("o (b s) -> (o b) s", s=BLOCK)
+        )
+        nc.sync.dma_start(
+            weight_rows[0:FIELD_BLOCKS, :], field.rearrange("o (b s) -> (o b) s", s=BLOCK)
+        )
         table = held.tile([C, S], F32, name="table")
         for k in range(S // LOAD):
             cols = slice(k * LOAD, (k + 1) * LOAD)
             nc.sync.dma_start(table[:, cols], x[:, cols])
         offsets = held.tile([C, N // 16], U16, name="offsets")
         nc.sync.dma_start(offsets[:], offs)
-        coup_vector = held.tile([C, VECTOR_PAIRS], F32, name="coup_vector")
-        nc.sync.dma_start(
-            coup_vector[:], coup.rearrange("o n -> (o n)")[N - VECTOR_PAIRS : N].partition_broadcast(C)
-        )
-
-        weight_rows = held.tile([C, BLOCK], F32, name="weight_rows")
-        nc.vector.memset(weight_rows[WEIGHT_BLOCKS:C, :], 0.0)
-        nc.scalar.dma_start(
-            weight_rows[0:FIELD_BLOCKS, :], field.rearrange("o (b s) -> (o b) s", s=BLOCK)
-        )
-        nc.scalar.dma_start(
-            weight_rows[FIELD_BLOCKS:WEIGHT_BLOCKS, :], coup.rearrange("o (b s) -> (o b) s", s=BLOCK)
-        )
-        bias_one = held.tile([1, 1], F32, name="bias_one")
-        nc.scalar.dma_start(bias_one[:], bias.unsqueeze(0))
+        bias_column = held.tile([C, 1], F32, name="bias_column")
+        nc.vector.memset(bias_column[:], 0.0)
+        nc.scalar.dma_start(bias_column[0:1, :], bias.unsqueeze(0))
 
         identity = held.tile([C, C], F32, name="identity")
-        make_identity(nc, identity[:])
+        unit = held.tile([C, C], F32, name="unit")
+        nc.vector.memset(unit[:], 1.0)
+        column_number = held.tile([C, C], F32, name="column_number", align_bytes=64)
+        nc.vector.tensor_tensor_scan(column_number[:], unit[:], unit[:], -1.0, MULT, ADD)
+        partition_number = held.tile([C, SQUARE], F32, name="partition_number", align_bytes=64)
+        nc.vector.transpose(partition_number[:], column_number[:, 0:SQUARE])
+        for first in range(SQUARE, C, SQUARE):
+            group = partition_number[first : first + SQUARE, 0:1]
+            nc.vector.tensor_scalar_add(group, group, float(first))
+        nc.vector.tensor_scalar(
+            identity[:], column_number[:], partition_number[:, 0:1], None, mybir.AluOpType.is_equal
+        )
+
         zeros = held.tile([C, C], F32, name="zeros")
         nc.vector.memset(zeros[:], 0.0)
-        ones = held.tile([C, 1], F32, name="ones")
-        nc.vector.memset(ones[:], 1.0)
+        energies = held.tile([C, SQUARE], F32, name="energies", align_bytes=64)
+        nc.vector.memset(energies[:], 0.0)
 
         weight_cols_ps = psum.tile([BLOCK, C], F32, name="weight_cols_ps")
         nc.tensor.transpose(weight_cols_ps[:], weight_rows[:], identity[:])
         weight_cols = held.tile([BLOCK, C], F32, name="weight_cols")
-        nc.scalar.activation(weight_cols[:], weight_cols_ps[:], IDENTITY)
+        nc.vector.tensor_copy(weight_cols[:], weight_cols_ps[:])
+
+        weighted_partners = held.tile([C, EARLIER + LATEST], F32, name="weighted_partners")
+        for u, first in enumerate(WEIGHTED_UNITS):
+            spread_ps = banks.tile([C, BANK], F32, name="flipped_ps")
+            for q in range(QUARTERS):
+                w = FIELD_BLOCKS + first // BLOCK + q
+                nc.tensor.transpose(
+                    spread_ps[:, q * BLOCK : (q + 1) * BLOCK],
+                    weight_cols[:, w : w + 1].to_broadcast([BLOCK, C]),
+                    identity[:],
+                )
+            nc.vector.tensor_tensor(
+                weighted_partners[:, u * BANK : (u + 1) * BANK],
+                spread_ps[:],
+                table[:, first % S : first % S + BANK],
+                MULT,
+            )
 
         partial = psum.tile([C, C], F32, name="partial")
         nc.tensor.matmul(partial[:], zeros[:], identity[:], start=True, stop=False)
 
         waiting = []
 
-        def weigh_waiting_round():
+        def weigh_waiting_round(last):
             for flipped, first_weight in waiting:
-                for q in range(QUARTERS):
-                    w = first_weight + q
+                blocks = flipped.shape[1] // BLOCK
+                for b in range(blocks):
+                    row = b % QUARTERS * QUARTER_ROWS
+                    w = first_weight + b
                     nc.tensor.matmul(
-                        partial[q * QUARTER_ROWS : q * QUARTER_ROWS + 1, :],
+                        partial[row : row + 1, :],
                         weight_cols[:, w : w + 1],
-                        flipped[:, q * BLOCK : (q + 1) * BLOCK],
+                        flipped[:, b * BLOCK : (b + 1) * BLOCK],
                         start=False,
-                        stop=(w >= TENSOR_BLOCKS - QUARTERS),
+                        stop=last and b >= blocks - QUARTERS,
                     )
             waiting.clear()
 
         def add_weighted_columns(values, first_weight):
-            flipped_round = []
+            flipped = stream.tile([BLOCK, CHUNK], F32, name="flipped")
             for g in range(values.shape[1] // BANK):
                 flipped_ps = banks.tile([BLOCK, BANK], F32, name="flipped_ps")
                 for q in range(QUARTERS):
@@ -98,51 +128,57 @@ def tile_linearpairwisemodule_kernel(tc, x, field, coup, bias, offs, out):
                         values[:, b * BLOCK : (b + 1) * BLOCK],
                         identity[:],
                     )
-                flipped = stream.tile([BLOCK, BANK], F32, name="flipped")
-                nc.scalar.activation(flipped[:], flipped_ps[:], IDENTITY)
-                flipped_round.append((flipped, first_weight + g * QUARTERS))
-            weigh_waiting_round()
-            waiting.extend(flipped_round)
+                nc.scalar.activation(
+                    flipped[:, g * BANK : (g + 1) * BANK], flipped_ps[:], IDENTITY
+                )
+            weigh_waiting_round(False)
+            waiting.append((flipped[:, 0 : values.shape[1]], first_weight))
+            return flipped
 
         partners = held.tile([C, S], F32, name="partners")
-        for k in range(S // CHUNK):
-            cols = slice(k * CHUNK, (k + 1) * CHUNK)
-            if (k + 1) * CHUNK <= S - LOAD:
-                nc.vector.tensor_copy(partners[:, cols], table[:, cols])
-            else:
+        for first in range(0, S, CHUNK):
+            cols = slice(first, first + CHUNK)
+            if first > 0:
                 nc.scalar.activation(partners[:, cols], table[:, cols], IDENTITY)
-            add_weighted_columns(table[:, cols], k * CHUNK // BLOCK)
+            add_weighted_columns(table[:, cols], first // BLOCK)
+        nc.scalar.activation(partners[:, BANK:CHUNK], table[:, BANK:CHUNK], IDENTITY)
 
-        products = held.tile([C, N], F32, name="products")
-        for p in range(N // PIECE):
-            pairs = slice(p * PIECE, (p + 1) * PIECE)
-            first = p * PIECE % S
-            picked = table[:].indirect(offsets[:, p * PIECE // 16 : (p + 1) * PIECE // 16])
-            nc.vector.tensor_tensor(
-                products[:, pairs], picked, partners[:, first : first + PIECE], MULT
+        def look_up(products, first, others):
+            count = products.shape[1]
+            picked = table[:].indirect(offsets[:, first // 16 : (first + count) // 16])
+            nc.vector.tensor_tensor(products, picked, others, MULT)
+
+        products = held.tile([C, PLAIN_PAIRS + 1], F32, name="products")
+        at = 0
+        for first, count in PLAIN:
+            partner = first % S
+            look_up(products[:, at : at + count], first, partners[:, partner : partner + count])
+            last_flipped = add_weighted_columns(
+                products[:, at : at + count], FIELD_BLOCKS + first // BLOCK
             )
-            if (p + 1) * PIECE <= N - VECTOR_PAIRS:
-                add_weighted_columns(products[:, pairs], FIELD_BLOCKS + p * PIECE // BLOCK)
-        weigh_waiting_round()
-        weighted = held.tile([C, VECTOR_PAIRS], F32, name="weighted")
-        vector_sum = held.tile([C, 1], F32, name="vector_sum")
-        nc.vector.scalar_tensor_tensor(
-            weighted[:],
-            products[:, N - VECTOR_PAIRS : N],
-            1.0,
-            coup_vector[:],
-            MULT,
-            MULT,
-            accum_out=vector_sum[:],
-        )
+            at += count
+        weigh_waiting_round(True)
+
+        earlier = products[:, 4 * CHUNK : 4 * CHUNK + EARLIER]
+        latest = products[:, PLAIN_PAIRS - LATEST : PLAIN_PAIRS + 1]
+        look_up(earlier, WEIGHTED_UNITS[0], weighted_partners[:, 0:EARLIER])
+        look_up(latest[:, 0:LATEST], WEIGHTED_UNITS[2], weighted_partners[:, EARLIER:])
 
         partial_sb = held.tile([C, C], F32, name="partial_sb")
-        nc.scalar.activation(partial_sb[:], partial[:], IDENTITY)
-        energy_row = psum.tile([1, C], F32, name="energy_row")
-        nc.tensor.matmul(energy_row[:], ones[:], partial_sb[:], start=True, stop=False)
-        nc.tensor.matmul(
-            energy_row[:], vector_sum[:], identity[:], start=False, stop=True, is_transpose=True
+        nc.scalar.activation(partial_sb[:], partial[:], IDENTITY, bias=bias_column[:, 0:1])
+        tensor_sum = psum.tile([C, 1], F32, name="tensor_sum")
+        nc.tensor.matmul(tensor_sum[:], partial_sb[:], unit[:, 0:1], start=True, stop=True)
+
+        nc.scalar.activation(
+            last_flipped[:, 0:EARLIER], earlier, IDENTITY, accum_out=latest[:, LATEST : LATEST + 1]
         )
-        energy = held.tile([1, C], F32, name="energy")
-        nc.vector.tensor_scalar_add(energy[:], energy_row[:], bias_one[:, 0:1])
-        nc.sync.dma_start(out.rearrange("c o -> o c"), energy[:])
+
+        added = held.tile([C, LATEST + 1], F32, name="added")
+        nc.vector.tensor_scalar(
+            added[:], latest, 1.0, tensor_sum[:, 0:1], MULT, ADD, accum_out=energies[:, 0:1]
+        )
+        energy_rows = held.tile([C, SQUARE], F32, name="energy_rows", align_bytes=64)
+        nc.vector.transpose(energy_rows[:], energies[:])
+        nc.sync.dma_start(
+            out.rearrange("(g r) o -> g (o r)", r=SQUARE), energy_rows[0:C:SQUARE, :]
+        )

@@ -12,6 +12,7 @@ C = 128
 S = 4096
 N = 8192
 LOAD = 2048
+ROUND = LOAD
 CHUNK = 1024
 BLOCK = 128
 BANK = 512
@@ -22,10 +23,15 @@ FIELD_BLOCKS = S // BLOCK
 COUP_BLOCKS = N // BLOCK
 WEIGHT_BLOCKS = FIELD_BLOCKS + COUP_BLOCKS
 
-WEIGHTED_UNITS = (0, BANK, S)
-EARLIER, LATEST = CHUNK, BANK
-PLAIN = [(k + c, CHUNK) for c in range(CHUNK, S, CHUNK) for k in range(0, N, S)] + [(S + BANK, BANK)]
-PLAIN_PAIRS = N - EARLIER - LATEST
+LATEST = 384
+WEIGHTED = [(0, CHUNK), (S, CHUNK - LATEST), (S + CHUNK - LATEST, LATEST)]
+PLAIN_ROUNDS = [
+    [(CHUNK, CHUNK), (S + CHUNK, CHUNK)],
+    [(2 * CHUNK, CHUNK), (S + 2 * CHUNK, CHUNK)],
+    [(3 * CHUNK, CHUNK)],
+    [(S + 3 * CHUNK, BANK), (S + 3 * CHUNK + BANK, BANK)],
+]
+SUMS = len(WEIGHTED)
 
 FLOPS = C * (2 * S + 3 * N)
 
@@ -59,19 +65,21 @@ def tile_linearpairwisemodule_kernel(tc, x, field, coup, bias, offs, out):
         identity = held.tile([C, C], F32, name="identity")
         unit = held.tile([C, C], F32, name="unit")
         nc.vector.memset(unit[:], 1.0)
-        column_number = held.tile([C, C], F32, name="column_number", align_bytes=64)
+        before = held.tile([C, 1], F32, name="before")
+        for first in range(0, C, SQUARE):
+            nc.vector.memset(before[first : first + SQUARE, :], first - 1.0)
+        counts = held.tile([C, SQUARE], F32, name="counts", align_bytes=64)
+        nc.vector.tensor_tensor_scan(
+            counts[:], unit[:, 0:SQUARE], unit[:, 0:SQUARE], before[:, 0:1], MULT, ADD
+        )
+        column_number = held.tile([C, C], F32, name="column_number")
         nc.vector.tensor_tensor_scan(column_number[:], unit[:], unit[:], -1.0, MULT, ADD)
         partition_number = held.tile([C, SQUARE], F32, name="partition_number", align_bytes=64)
-        nc.vector.transpose(partition_number[:], column_number[:, 0:SQUARE])
-        for first in range(SQUARE, C, SQUARE):
-            group = partition_number[first : first + SQUARE, 0:1]
-            nc.vector.tensor_scalar_add(group, group, float(first))
+        nc.vector.transpose(partition_number[:], counts[:])
         nc.vector.tensor_scalar(
-            identity[:], column_number[:], partition_number[:, 0:1], None, mybir.AluOpType.is_equal
+            identity[:], column_number[:], partition_number[:, 0:1], None, IS_EQUAL
         )
 
-        zeros = held.tile([C, C], F32, name="zeros")
-        nc.vector.memset(zeros[:], 0.0)
         energies = held.tile([C, SQUARE], F32, name="energies", align_bytes=64)
         nc.vector.memset(energies[:], 0.0)
 
@@ -80,8 +88,9 @@ def tile_linearpairwisemodule_kernel(tc, x, field, coup, bias, offs, out):
         weight_cols = held.tile([BLOCK, C], F32, name="weight_cols")
         nc.vector.tensor_copy(weight_cols[:], weight_cols_ps[:])
 
-        weighted_partners = held.tile([C, EARLIER + LATEST], F32, name="weighted_partners")
-        for u, first in enumerate(WEIGHTED_UNITS):
+        weighted_partners = held.tile([C, N // S * CHUNK], F32, name="weighted_partners")
+        units = [k + u for k in range(0, N, S) for u in range(0, CHUNK, BANK)]
+        for u, first in enumerate(units):
             spread_ps = banks.tile([C, BANK], F32, name="flipped_ps")
             for q in range(QUARTERS):
                 w = FIELD_BLOCKS + first // BLOCK + q
@@ -97,13 +106,14 @@ def tile_linearpairwisemodule_kernel(tc, x, field, coup, bias, offs, out):
                 MULT,
             )
 
+        nc.vector.memset(weight_rows[:], 0.0)
         partial = psum.tile([C, C], F32, name="partial")
-        nc.tensor.matmul(partial[:], zeros[:], identity[:], start=True, stop=False)
+        nc.tensor.matmul(partial[:], weight_rows[:], identity[:], start=True, stop=False)
 
         waiting = []
 
         def weigh_waiting_round(last):
-            for flipped, first_weight in waiting:
+            for i, (flipped, first_weight) in enumerate(waiting):
                 blocks = flipped.shape[1] // BLOCK
                 for b in range(blocks):
                     row = b % QUARTERS * QUARTER_ROWS
@@ -113,70 +123,80 @@ def tile_linearpairwisemodule_kernel(tc, x, field, coup, bias, offs, out):
                         weight_cols[:, w : w + 1],
                         flipped[:, b * BLOCK : (b + 1) * BLOCK],
                         start=False,
-                        stop=last and b >= blocks - QUARTERS,
+                        stop=last and i == len(waiting) - 1 and b >= blocks - QUARTERS,
                     )
             waiting.clear()
 
-        def add_weighted_columns(values, first_weight):
-            flipped = stream.tile([BLOCK, CHUNK], F32, name="flipped")
-            for g in range(values.shape[1] // BANK):
-                flipped_ps = banks.tile([BLOCK, BANK], F32, name="flipped_ps")
-                for q in range(QUARTERS):
-                    b = g * QUARTERS + q
-                    nc.tensor.transpose(
-                        flipped_ps[:, q * BLOCK : (q + 1) * BLOCK],
-                        values[:, b * BLOCK : (b + 1) * BLOCK],
-                        identity[:],
+        def add_weighted_columns(parts, first_weights):
+            flipped = stream.tile([BLOCK, ROUND], F32, name="flipped")
+            flipped_parts = []
+            at = 0
+            for values, first_weight in zip(parts, first_weights):
+                count = values.shape[1]
+                for unit_start in range(0, count, BANK):
+                    flipped_ps = banks.tile([BLOCK, BANK], F32, name="flipped_ps")
+                    for q in range(QUARTERS):
+                        v = unit_start + q * BLOCK
+                        nc.tensor.transpose(
+                            flipped_ps[:, q * BLOCK : (q + 1) * BLOCK],
+                            values[:, v : v + BLOCK],
+                            identity[:],
+                        )
+                    nc.scalar.activation(
+                        flipped[:, at + unit_start : at + unit_start + BANK],
+                        flipped_ps[:],
+                        IDENTITY,
                     )
-                nc.scalar.activation(
-                    flipped[:, g * BANK : (g + 1) * BANK], flipped_ps[:], IDENTITY
-                )
+                flipped_parts.append((flipped[:, at : at + count], first_weight))
+                at += count
             weigh_waiting_round(False)
-            waiting.append((flipped[:, 0 : values.shape[1]], first_weight))
-            return flipped
+            waiting.extend(flipped_parts)
 
         partners = held.tile([C, S], F32, name="partners")
-        for first in range(0, S, CHUNK):
-            cols = slice(first, first + CHUNK)
-            if first > 0:
-                nc.scalar.activation(partners[:, cols], table[:, cols], IDENTITY)
-            add_weighted_columns(table[:, cols], first // BLOCK)
-        nc.scalar.activation(partners[:, BANK:CHUNK], table[:, BANK:CHUNK], IDENTITY)
+        for first in range(0, S, ROUND):
+            for c in range(max(first, CHUNK), first + ROUND, CHUNK):
+                nc.scalar.activation(partners[:, c : c + CHUNK], table[:, c : c + CHUNK], IDENTITY)
+            add_weighted_columns([table[:, first : first + ROUND]], [first // BLOCK])
 
         def look_up(products, first, others):
             count = products.shape[1]
             picked = table[:].indirect(offsets[:, first // 16 : (first + count) // 16])
             nc.vector.tensor_tensor(products, picked, others, MULT)
 
-        products = held.tile([C, PLAIN_PAIRS + 1], F32, name="products")
-        at = 0
-        for first, count in PLAIN:
-            partner = first % S
-            look_up(products[:, at : at + count], first, partners[:, partner : partner + count])
-            last_flipped = add_weighted_columns(
-                products[:, at : at + count], FIELD_BLOCKS + first // BLOCK
-            )
-            at += count
+        plain = []
+        for look_ups in PLAIN_ROUNDS:
+            parts = []
+            for first, count in look_ups:
+                products = held.tile([C, CHUNK + SUMS], F32, name=f"products_{first}")
+                partner = first % S
+                look_up(products[:, 0:count], first, partners[:, partner : partner + count])
+                plain.append(products)
+                parts.append(products[:, 0:count])
+            add_weighted_columns(parts, [FIELD_BLOCKS + first // BLOCK for first, count in look_ups])
         weigh_waiting_round(True)
 
-        earlier = products[:, 4 * CHUNK : 4 * CHUNK + EARLIER]
-        latest = products[:, PLAIN_PAIRS - LATEST : PLAIN_PAIRS + 1]
-        look_up(earlier, WEIGHTED_UNITS[0], weighted_partners[:, 0:EARLIER])
-        look_up(latest[:, 0:LATEST], WEIGHTED_UNITS[2], weighted_partners[:, EARLIER:])
+        latest = plain[-2][:, BANK - LATEST : BANK + SUMS]
+        places = [plain[-4][:, 0:CHUNK], plain[-3][:, 0 : CHUNK - LATEST], latest[:, 0:LATEST]]
+        at = 0
+        for place, (first, count) in zip(places, WEIGHTED):
+            look_up(place, first, weighted_partners[:, at : at + count])
+            at += count
+
+        for u, place in enumerate(places[:-1]):
+            nc.scalar.activation(
+                plain[-1][:, 0 : place.shape[1]],
+                place,
+                IDENTITY,
+                accum_out=latest[:, LATEST + u : LATEST + u + 1],
+            )
 
         partial_sb = held.tile([C, C], F32, name="partial_sb")
         nc.scalar.activation(partial_sb[:], partial[:], IDENTITY, bias=bias_column[:, 0:1])
         tensor_sum = psum.tile([C, 1], F32, name="tensor_sum")
         nc.tensor.matmul(tensor_sum[:], partial_sb[:], unit[:, 0:1], start=True, stop=True)
+        nc.scalar.activation(latest[:, LATEST + SUMS - 1 :], tensor_sum[:], IDENTITY)
 
-        nc.scalar.activation(
-            last_flipped[:, 0:EARLIER], earlier, IDENTITY, accum_out=latest[:, LATEST : LATEST + 1]
-        )
-
-        added = held.tile([C, LATEST + 1], F32, name="added")
-        nc.vector.tensor_scalar(
-            added[:], latest, 1.0, tensor_sum[:, 0:1], MULT, ADD, accum_out=energies[:, 0:1]
-        )
+        nc.vector.tensor_reduce(energies[:, 0:1], latest, AXIS_X, ADD)
         energy_rows = held.tile([C, SQUARE], F32, name="energy_rows", align_bytes=64)
         nc.vector.transpose(energy_rows[:], energies[:])
         nc.sync.dma_start(

@@ -21,10 +21,11 @@ QUARTER_ROWS = C // QUARTERS
 SQUARE = 32
 FIELD_BLOCKS = S // BLOCK
 COUP_BLOCKS = N // BLOCK
-WEIGHT_BLOCKS = FIELD_BLOCKS + COUP_BLOCKS
+WEIGHT_BLOCKS = COUP_BLOCKS + FIELD_BLOCKS
+PASSES = N // S
 
 LATEST = 384
-WEIGHTED = [(0, CHUNK), (S, CHUNK - LATEST), (S + CHUNK - LATEST, LATEST)]
+WEIGHTED = [(0, BANK), (BANK, BANK), (S, CHUNK - LATEST), (S + CHUNK - LATEST, LATEST)]
 PLAIN_ROUNDS = [
     [(CHUNK, CHUNK), (S + CHUNK, CHUNK)],
     [(2 * CHUNK, CHUNK), (S + 2 * CHUNK, CHUNK)],
@@ -44,20 +45,16 @@ def tile_linearpairwisemodule_kernel(tc, x, field, coup, bias, offs, out):
         tc.psum_pool(name="psum", bufs=1) as psum,
         tc.psum_pool(name="banks", bufs=2 * CHUNK // BANK) as banks,
     ):
-        weight_rows = held.tile([C, BLOCK], F32, name="weight_rows")
-        nc.vector.memset(weight_rows[WEIGHT_BLOCKS:C, :], 0.0)
-        nc.sync.dma_start(
-            weight_rows[FIELD_BLOCKS:WEIGHT_BLOCKS, :], coup.rearrange("o (b s) -> (o b) s", s=BLOCK)
-        )
-        nc.sync.dma_start(
-            weight_rows[0:FIELD_BLOCKS, :], field.rearrange("o (b s) -> (o b) s", s=BLOCK)
-        )
+        coup_rows = held.tile([COUP_BLOCKS, BLOCK], F32, name="coup_rows")
+        nc.sync.dma_start(coup_rows[:], coup.rearrange("o (b s) -> (o b) s", s=BLOCK))
         table = held.tile([C, S], F32, name="table")
         for k in range(S // LOAD):
             cols = slice(k * LOAD, (k + 1) * LOAD)
             nc.sync.dma_start(table[:, cols], x[:, cols])
         offsets = held.tile([C, N // 16], U16, name="offsets")
         nc.sync.dma_start(offsets[:], offs)
+        field_rows = held.tile([FIELD_BLOCKS, BLOCK], F32, name="field_rows")
+        nc.scalar.dma_start(field_rows[:], field.rearrange("o (b s) -> (o b) s", s=BLOCK))
         bias_column = held.tile([C, 1], F32, name="bias_column")
         nc.vector.memset(bias_column[:], 0.0)
         nc.scalar.dma_start(bias_column[0:1, :], bias.unsqueeze(0))
@@ -83,17 +80,20 @@ def tile_linearpairwisemodule_kernel(tc, x, field, coup, bias, offs, out):
         energies = held.tile([C, SQUARE], F32, name="energies", align_bytes=64)
         nc.vector.memset(energies[:], 0.0)
 
-        weight_cols_ps = psum.tile([BLOCK, C], F32, name="weight_cols_ps")
-        nc.tensor.transpose(weight_cols_ps[:], weight_rows[:], identity[:])
+        weight_cols_ps = psum.tile([BLOCK, WEIGHT_BLOCKS], F32, name="weight_cols_ps")
         weight_cols = held.tile([BLOCK, C], F32, name="weight_cols")
-        nc.vector.tensor_copy(weight_cols[:], weight_cols_ps[:])
-
-        weighted_partners = held.tile([C, N // S * CHUNK], F32, name="weighted_partners")
-        units = [k + u for k in range(0, N, S) for u in range(0, CHUNK, BANK)]
-        for u, first in enumerate(units):
+        nc.vector.memset(weight_cols[:, WEIGHT_BLOCKS:C], 0.0)
+        nc.tensor.transpose(
+            weight_cols_ps[:, 0:COUP_BLOCKS], coup_rows[:], identity[0:COUP_BLOCKS, 0:COUP_BLOCKS]
+        )
+        nc.vector.tensor_copy(weight_cols[:, 0:COUP_BLOCKS], weight_cols_ps[:, 0:COUP_BLOCKS])
+        weighted_partners = held.tile([C, PASSES * CHUNK], F32, name="weighted_partners")
+        for u in range(PASSES * CHUNK // BANK):
+            column = u * BANK % CHUNK
+            first_weight = (u * BANK // CHUNK * S + column) // BLOCK
             spread_ps = banks.tile([C, BANK], F32, name="flipped_ps")
             for q in range(QUARTERS):
-                w = FIELD_BLOCKS + first // BLOCK + q
+                w = first_weight + q
                 nc.tensor.transpose(
                     spread_ps[:, q * BLOCK : (q + 1) * BLOCK],
                     weight_cols[:, w : w + 1].to_broadcast([BLOCK, C]),
@@ -102,13 +102,24 @@ def tile_linearpairwisemodule_kernel(tc, x, field, coup, bias, offs, out):
             nc.vector.tensor_tensor(
                 weighted_partners[:, u * BANK : (u + 1) * BANK],
                 spread_ps[:],
-                table[:, first % S : first % S + BANK],
+                table[:, column : column + BANK],
                 MULT,
             )
 
-        nc.vector.memset(weight_rows[:], 0.0)
+        field_cols = slice(COUP_BLOCKS, WEIGHT_BLOCKS)
+        nc.tensor.matmul(
+            weight_cols_ps[:, field_cols],
+            field_rows[:],
+            identity[0:FIELD_BLOCKS, 0:FIELD_BLOCKS],
+            start=True,
+            stop=True,
+        )
+        nc.scalar.activation(weight_cols[:, field_cols], weight_cols_ps[:, field_cols], IDENTITY)
+
+        zeros = held.tile([C, C], F32, name="zeros")
+        nc.vector.memset(zeros[:], 0.0)
         partial = psum.tile([C, C], F32, name="partial")
-        nc.tensor.matmul(partial[:], weight_rows[:], identity[:], start=True, stop=False)
+        nc.tensor.matmul(partial[:], zeros[:], weight_cols[:], start=True, stop=False)
 
         waiting = []
 
@@ -156,7 +167,7 @@ def tile_linearpairwisemodule_kernel(tc, x, field, coup, bias, offs, out):
         for first in range(0, S, ROUND):
             for c in range(max(first, CHUNK), first + ROUND, CHUNK):
                 nc.scalar.activation(partners[:, c : c + CHUNK], table[:, c : c + CHUNK], IDENTITY)
-            add_weighted_columns([table[:, first : first + ROUND]], [first // BLOCK])
+            add_weighted_columns([table[:, first : first + ROUND]], [COUP_BLOCKS + first // BLOCK])
 
         def look_up(products, first, others):
             count = products.shape[1]
@@ -172,29 +183,37 @@ def tile_linearpairwisemodule_kernel(tc, x, field, coup, bias, offs, out):
                 look_up(products[:, 0:count], first, partners[:, partner : partner + count])
                 plain.append(products)
                 parts.append(products[:, 0:count])
-            add_weighted_columns(parts, [FIELD_BLOCKS + first // BLOCK for first, count in look_ups])
+            add_weighted_columns(parts, [first // BLOCK for first, count in look_ups])
         weigh_waiting_round(True)
 
         latest = plain[-2][:, BANK - LATEST : BANK + SUMS]
-        places = [plain[-4][:, 0:CHUNK], plain[-3][:, 0 : CHUNK - LATEST], latest[:, 0:LATEST]]
+        places = [
+            plain[2][:, 0:BANK],
+            plain[2][:, BANK:CHUNK],
+            plain[3][:, 0 : CHUNK - LATEST],
+            latest[:, 0:LATEST],
+        ]
         at = 0
         for place, (first, count) in zip(places, WEIGHTED):
             look_up(place, first, weighted_partners[:, at : at + count])
             at += count
 
-        for u, place in enumerate(places[:-1]):
+        def sum_products(u):
             nc.scalar.activation(
-                plain[-1][:, 0 : place.shape[1]],
-                place,
+                plain[-1][:, 0 : places[u].shape[1]],
+                places[u],
                 IDENTITY,
                 accum_out=latest[:, LATEST + u : LATEST + u + 1],
             )
 
+        sum_products(0)
         partial_sb = held.tile([C, C], F32, name="partial_sb")
         nc.scalar.activation(partial_sb[:], partial[:], IDENTITY, bias=bias_column[:, 0:1])
         tensor_sum = psum.tile([C, 1], F32, name="tensor_sum")
         nc.tensor.matmul(tensor_sum[:], partial_sb[:], unit[:, 0:1], start=True, stop=True)
         nc.scalar.activation(latest[:, LATEST + SUMS - 1 :], tensor_sum[:], IDENTITY)
+        for u in range(1, len(WEIGHTED) - 1):
+            sum_products(u)
 
         nc.vector.tensor_reduce(energies[:, 0:1], latest, AXIS_X, ADD)
         energy_rows = held.tile([C, SQUARE], F32, name="energy_rows", align_bytes=64)

@@ -25,7 +25,7 @@ WEIGHT_BLOCKS = COUP_BLOCKS + FIELD_BLOCKS
 PASSES = N // S
 
 LATEST = 384
-WEIGHTED = [(0, BANK), (BANK, BANK), (S, CHUNK - LATEST), (S + CHUNK - LATEST, LATEST)]
+WEIGHTED = [(0, CHUNK), (S, CHUNK - LATEST), (S + CHUNK - LATEST, LATEST)]
 PLAIN_ROUNDS = [
     [(CHUNK, CHUNK), (S + CHUNK, CHUNK)],
     [(2 * CHUNK, CHUNK), (S + 2 * CHUNK, CHUNK)],
@@ -188,8 +188,7 @@ def tile_linearpairwisemodule_kernel(tc, x, field, coup, bias, offs, out):
 
         latest = plain[-2][:, BANK - LATEST : BANK + SUMS]
         places = [
-            plain[2][:, 0:BANK],
-            plain[2][:, BANK:CHUNK],
+            plain[2][:, 0:CHUNK],
             plain[3][:, 0 : CHUNK - LATEST],
             latest[:, 0:LATEST],
         ]

@@ -6,7 +6,6 @@ MULT = mybir.AluOpType.mult
 ADD = mybir.AluOpType.add
 IS_EQUAL = mybir.AluOpType.is_equal
 IDENTITY = mybir.ActivationFunctionType.Identity
-AXIS_X = mybir.AxisListType.X
 
 C = 128
 S = 4096
@@ -24,15 +23,16 @@ COUP_BLOCKS = N // BLOCK
 WEIGHT_BLOCKS = COUP_BLOCKS + FIELD_BLOCKS
 PASSES = N // S
 
-LATEST = 384
-WEIGHTED = [(0, CHUNK), (S, CHUNK - LATEST), (S + CHUNK - LATEST, LATEST)]
+EARLIER = 640
+WEIGHTED = [(0, EARLIER), (EARLIER, CHUNK - EARLIER), (S, BANK)]
+SUMS = len(WEIGHTED) - 1
 PLAIN_ROUNDS = [
     [(CHUNK, CHUNK), (S + CHUNK, CHUNK)],
     [(2 * CHUNK, CHUNK), (S + 2 * CHUNK, CHUNK)],
     [(3 * CHUNK, CHUNK)],
-    [(S + 3 * CHUNK, BANK), (S + 3 * CHUNK + BANK, BANK)],
+    [(S + 3 * CHUNK, CHUNK)],
+    [(S + BANK, BANK)],
 ]
-SUMS = len(WEIGHTED)
 
 FLOPS = C * (2 * S + 3 * N)
 
@@ -87,8 +87,8 @@ def tile_linearpairwisemodule_kernel(tc, x, field, coup, bias, offs, out):
             weight_cols_ps[:, 0:COUP_BLOCKS], coup_rows[:], identity[0:COUP_BLOCKS, 0:COUP_BLOCKS]
         )
         nc.vector.tensor_copy(weight_cols[:, 0:COUP_BLOCKS], weight_cols_ps[:, 0:COUP_BLOCKS])
-        weighted_partners = held.tile([C, PASSES * CHUNK], F32, name="weighted_partners")
-        for u in range(PASSES * CHUNK // BANK):
+        weighted_partners = held.tile([C, CHUNK + BANK], F32, name="weighted_partners")
+        for u in range((CHUNK + BANK) // BANK):
             column = u * BANK % CHUNK
             first_weight = (u * BANK // CHUNK * S + column) // BLOCK
             spread_ps = banks.tile([C, BANK], F32, name="flipped_ps")
@@ -105,6 +105,9 @@ def tile_linearpairwisemodule_kernel(tc, x, field, coup, bias, offs, out):
                 table[:, column : column + BANK],
                 MULT,
             )
+
+        partners = held.tile([C, S], F32, name="partners")
+        nc.scalar.activation(partners[:, CHUNK : 2 * CHUNK], table[:, CHUNK : 2 * CHUNK], IDENTITY)
 
         field_cols = slice(COUP_BLOCKS, WEIGHT_BLOCKS)
         nc.tensor.matmul(
@@ -163,11 +166,11 @@ def tile_linearpairwisemodule_kernel(tc, x, field, coup, bias, offs, out):
             weigh_waiting_round(False)
             waiting.extend(flipped_parts)
 
-        partners = held.tile([C, S], F32, name="partners")
         for first in range(0, S, ROUND):
-            for c in range(max(first, CHUNK), first + ROUND, CHUNK):
+            for c in range(max(first, 2 * CHUNK), first + ROUND, CHUNK):
                 nc.scalar.activation(partners[:, c : c + CHUNK], table[:, c : c + CHUNK], IDENTITY)
             add_weighted_columns([table[:, first : first + ROUND]], [COUP_BLOCKS + first // BLOCK])
+        nc.scalar.activation(partners[:, BANK:CHUNK], table[:, BANK:CHUNK], IDENTITY)
 
         def look_up(products, first, others):
             count = products.shape[1]
@@ -186,12 +189,8 @@ def tile_linearpairwisemodule_kernel(tc, x, field, coup, bias, offs, out):
             add_weighted_columns(parts, [first // BLOCK for first, count in look_ups])
         weigh_waiting_round(True)
 
-        latest = plain[-2][:, BANK - LATEST : BANK + SUMS]
-        places = [
-            plain[2][:, 0:CHUNK],
-            plain[3][:, 0 : CHUNK - LATEST],
-            latest[:, 0:LATEST],
-        ]
+        latest = plain[-2][:, CHUNK - BANK : CHUNK + SUMS]
+        places = [plain[2][:, 0:EARLIER], plain[3][:, 0 : CHUNK - EARLIER], latest[:, 0:BANK]]
         at = 0
         for place, (first, count) in zip(places, WEIGHTED):
             look_up(place, first, weighted_partners[:, at : at + count])
@@ -202,7 +201,7 @@ def tile_linearpairwisemodule_kernel(tc, x, field, coup, bias, offs, out):
                 plain[-1][:, 0 : places[u].shape[1]],
                 places[u],
                 IDENTITY,
-                accum_out=latest[:, LATEST + u : LATEST + u + 1],
+                accum_out=latest[:, BANK + u : BANK + u + 1],
             )
 
         sum_products(0)
@@ -210,11 +209,12 @@ def tile_linearpairwisemodule_kernel(tc, x, field, coup, bias, offs, out):
         nc.scalar.activation(partial_sb[:], partial[:], IDENTITY, bias=bias_column[:, 0:1])
         tensor_sum = psum.tile([C, 1], F32, name="tensor_sum")
         nc.tensor.matmul(tensor_sum[:], partial_sb[:], unit[:, 0:1], start=True, stop=True)
-        nc.scalar.activation(latest[:, LATEST + SUMS - 1 :], tensor_sum[:], IDENTITY)
-        for u in range(1, len(WEIGHTED) - 1):
-            sum_products(u)
+        sum_products(1)
 
-        nc.vector.tensor_reduce(energies[:, 0:1], latest, AXIS_X, ADD)
+        added = held.tile([C, BANK + SUMS], F32, name="added")
+        nc.vector.tensor_scalar(
+            added[:], latest, 1.0, tensor_sum[:, 0:1], MULT, ADD, accum_out=energies[:, 0:1]
+        )
         energy_rows = held.tile([C, SQUARE], F32, name="energy_rows", align_bytes=64)
         nc.vector.transpose(energy_rows[:], energies[:])
         nc.sync.dma_start(

@@ -23,8 +23,8 @@ COUP_BLOCKS = N // BLOCK
 WEIGHT_BLOCKS = COUP_BLOCKS + FIELD_BLOCKS
 PASSES = N // S
 
-EARLIER = 640
-WEIGHTED = [(0, EARLIER), (EARLIER, CHUNK - EARLIER), (S, BANK)]
+LATEST = 384
+WEIGHTED = [(S, BANK), (0, CHUNK - LATEST), (CHUNK - LATEST, LATEST)]
 SUMS = len(WEIGHTED) - 1
 PLAIN_ROUNDS = [
     [(CHUNK, CHUNK), (S + CHUNK, CHUNK)],
@@ -54,7 +54,7 @@ def tile_linearpairwisemodule_kernel(tc, x, field, coup, bias, offs, out):
         offsets = held.tile([C, N // 16], U16, name="offsets")
         nc.sync.dma_start(offsets[:], offs)
         field_rows = held.tile([FIELD_BLOCKS, BLOCK], F32, name="field_rows")
-        nc.scalar.dma_start(field_rows[:], field.rearrange("o (b s) -> (o b) s", s=BLOCK))
+        nc.sync.dma_start(field_rows[:], field.rearrange("o (b s) -> (o b) s", s=BLOCK))
         bias_column = held.tile([C, 1], F32, name="bias_column")
         nc.vector.memset(bias_column[:], 0.0)
         nc.scalar.dma_start(bias_column[0:1, :], bias.unsqueeze(0))
@@ -189,19 +189,18 @@ def tile_linearpairwisemodule_kernel(tc, x, field, coup, bias, offs, out):
             add_weighted_columns(parts, [first // BLOCK for first, count in look_ups])
         weigh_waiting_round(True)
 
-        latest = plain[-2][:, CHUNK - BANK : CHUNK + SUMS]
-        places = [plain[2][:, 0:EARLIER], plain[3][:, 0 : CHUNK - EARLIER], latest[:, 0:BANK]]
-        at = 0
+        latest = plain[-2][:, CHUNK - LATEST : CHUNK + SUMS]
+        places = [plain[2][:, 0:BANK], plain[3][:, 0 : CHUNK - LATEST], latest[:, 0:LATEST]]
         for place, (first, count) in zip(places, WEIGHTED):
+            at = first // S * CHUNK + first % S
             look_up(place, first, weighted_partners[:, at : at + count])
-            at += count
 
         def sum_products(u):
             nc.scalar.activation(
                 plain[-1][:, 0 : places[u].shape[1]],
                 places[u],
                 IDENTITY,
-                accum_out=latest[:, BANK + u : BANK + u + 1],
+                accum_out=latest[:, LATEST + u : LATEST + u + 1],
             )
 
         sum_products(0)
@@ -211,7 +210,7 @@ def tile_linearpairwisemodule_kernel(tc, x, field, coup, bias, offs, out):
         nc.tensor.matmul(tensor_sum[:], partial_sb[:], unit[:, 0:1], start=True, stop=True)
         sum_products(1)
 
-        added = held.tile([C, BANK + SUMS], F32, name="added")
+        added = held.tile([C, LATEST + SUMS], F32, name="added")
         nc.vector.tensor_scalar(
             added[:], latest, 1.0, tensor_sum[:, 0:1], MULT, ADD, accum_out=energies[:, 0:1]
         )

import concourse.mybir as mybir

F32 = mybir.dt.float32
U16 = mybir.dt.uint16
MULT = mybir.AluOpType.mult
ADD = mybir.AluOpType.add
IS_EQUAL = mybir.AluOpType.is_equal
IDENTITY = mybir.ActivationFunctionType.Identity

C = 128
S = 4096
N = 8192
LOAD = 2048
ROUND = LOAD
CHUNK = 1024
BLOCK = 128
BANK = 512
QUARTERS = BANK // BLOCK
QUARTER_ROWS = C // QUARTERS
SQUARE = 32
FIELD_BLOCKS = S // BLOCK
COUP_BLOCKS = N // BLOCK
WEIGHT_BLOCKS = COUP_BLOCKS + FIELD_BLOCKS
PASSES = N // S

LATEST = 384
WEIGHTED = [(S, BANK), (0, CHUNK - LATEST), (CHUNK - LATEST, LATEST)]
SUMS = len(WEIGHTED) - 1
PLAIN_ROUNDS = [
    [(CHUNK, CHUNK), (S + CHUNK, CHUNK)],
    [(2 * CHUNK, CHUNK), (S + 2 * CHUNK, CHUNK)],
    [(3 * CHUNK, CHUNK)],
    [(S + 3 * CHUNK, CHUNK)],
    [(S + BANK, BANK)],
]

FLOPS = C * (2 * S + 3 * N)


def tile_linearpairwisemodule_kernel(tc, x, field, coup, bias, offs, out):
    nc = tc.nc
    with (
        tc.tile_pool(name="held", bufs=1) as held,
        tc.tile_pool(name="stream", bufs=3) as stream,
        tc.psum_pool(name="psum", bufs=1) as psum,
        tc.psum_pool(name="banks", bufs=2 * CHUNK // BANK) as banks,
    ):
        coup_rows = held.tile([COUP_BLOCKS, BLOCK], F32, name="coup_rows")
        nc.sync.dma_start(coup_rows[:], coup.rearrange("o (b s) -> (o b) s", s=BLOCK))
        table = held.tile([C, S], F32, name="table")
        for k in range(S // LOAD):
            cols = slice(k * LOAD, (k + 1) * LOAD)
            nc.sync.dma_start(table[:, cols], x[:, cols])
        offsets = held.tile([C, N // 16], U16, name="offsets")
        nc.sync.dma_start(offsets[:], offs)
        field_rows = held.tile([FIELD_BLOCKS, BLOCK], F32, name="field_rows")
        nc.sync.dma_start(field_rows[:], field.rearrange("o (b s) -> (o b) s", s=BLOCK))
        bias_column = held.tile([C, 1], F32, name="bias_column")
        nc.vector.memset(bias_column[:], 0.0)
        nc.scalar.dma_start(bias_column[0:1, :], bias.unsqueeze(0))

        identity = held.tile([C, C], F32, name="identity")
        unit = held.tile([C, C], F32, name="unit")
        nc.vector.memset(unit[:], 1.0)
        before = held.tile([C, 1], F32, name="before")
        for first in range(0, C, SQUARE):
            nc.vector.memset(before[first : first + SQUARE, :], first - 1.0)
        counts = held.tile([C, SQUARE], F32, name="counts", align_bytes=64)
        nc.vector.tensor_tensor_scan(
            counts[:], unit[:, 0:SQUARE], unit[:, 0:SQUARE], before[:, 0:1], MULT, ADD
        )
        column_number = held.tile([C, C], F32, name="column_number")
        nc.vector.tensor_tensor_scan(column_number[:], unit[:], unit[:], -1.0, MULT, ADD)
        partition_number = held.tile([C, SQUARE], F32, name="partition_number", align_bytes=64)
        nc.vector.transpose(partition_number[:], counts[:])
        nc.vector.tensor_scalar(
            identity[:], column_number[:], partition_number[:, 0:1], None, IS_EQUAL
        )

        energies = held.tile([C, SQUARE], F32, name="energies", align_bytes=64)
        nc.vector.memset(energies[:], 0.0)

        weight_cols_ps = psum.tile([BLOCK, WEIGHT_BLOCKS], F32, name="weight_cols_ps")
        weight_cols = held.tile([BLOCK, C], F32, name="weight_cols")
        nc.vector.memset(weight_cols[:, WEIGHT_BLOCKS:C], 0.0)
        nc.tensor.transpose(
            weight_cols_ps[:, 0:COUP_BLOCKS], coup_rows[:], identity[0:COUP_BLOCKS, 0:COUP_BLOCKS]
        )
        nc.vector.tensor_copy(weight_cols[:, 0:COUP_BLOCKS], weight_cols_ps[:, 0:COUP_BLOCKS])
        weighted_partners = held.tile([C, CHUNK + BANK], F32, name="weighted_partners")
        for u in range((CHUNK + BANK) // BANK):
            column = u * BANK % CHUNK
            first_weight = (u * BANK // CHUNK * S + column) // BLOCK
            spread_ps = banks.tile([C, BANK], F32, name="flipped_ps")
            for q in range(QUARTERS):
                w = first_weight + q
                nc.tensor.transpose(
                    spread_ps[:, q * BLOCK : (q + 1) * BLOCK],
                    weight_cols[:, w : w + 1].to_broadcast([BLOCK, C]),
                    identity[:],
                )
            nc.vector.tensor_tensor(
                weighted_partners[:, u * BANK : (u + 1) * BANK],
                spread_ps[:],
                table[:, column : column + BANK],
                MULT,
            )

        partners = held.tile([C, S], F32, name="partners")
        nc.scalar.activation(partners[:, CHUNK : 2 * CHUNK], table[:, CHUNK : 2 * CHUNK], IDENTITY)

        field_cols = slice(COUP_BLOCKS, WEIGHT_BLOCKS)
        nc.tensor.matmul(
            weight_cols_ps[:, field_cols],
            field_rows[:],
            identity[0:FIELD_BLOCKS, 0:FIELD_BLOCKS],
            start=True,
            stop=True,
        )
        nc.scalar.activation(weight_cols[:, field_cols], weight_cols_ps[:, field_cols], IDENTITY)

        zeros = held.tile([C, C], F32, name="zeros")
        nc.vector.memset(zeros[:], 0.0)
        partial = psum.tile([C, C], F32, name="partial")
        nc.tensor.matmul(partial[:], zeros[:], weight_cols[:], start=True, stop=False)

        waiting = []

        def weigh_waiting_round(last):
            for i, (flipped, first_weight) in enumerate(waiting):
                blocks = flipped.shape[1] // BLOCK
                for b in range(blocks):
                    row = b % QUARTERS * QUARTER_ROWS
                    w = first_weight + b
                    nc.tensor.matmul(
                        partial[row : row + 1, :],
                        weight_cols[:, w : w + 1],
                        flipped[:, b * BLOCK : (b + 1) * BLOCK],
                        start=False,
                        stop=last and i == len(waiting) - 1 and b >= blocks - QUARTERS,
                    )
            waiting.clear()

        def add_weighted_columns(parts, first_weights):
            flipped = stream.tile([BLOCK, ROUND], F32, name="flipped")
            flipped_parts = []
            at = 0
            for values, first_weight in zip(parts, first_weights):
                count = values.shape[1]
                for unit_start in range(0, count, BANK):
                    flipped_ps = banks.tile([BLOCK, BANK], F32, name="flipped_ps")
                    for q in range(QUARTERS):
                        v = unit_start + q * BLOCK
                        nc.tensor.transpose(
                            flipped_ps[:, q * BLOCK : (q + 1) * BLOCK],
                            values[:, v : v + BLOCK],
                            identity[:],
                        )
                    nc.scalar.activation(
                        flipped[:, at + unit_start : at + unit_start + BANK],
                        flipped_ps[:],
                        IDENTITY,
                    )
                flipped_parts.append((flipped[:, at : at + count], first_weight))
                at += count
            weigh_waiting_round(False)
            waiting.extend(flipped_parts)

        for first in range(0, S, ROUND):
            for c in range(max(first, 2 * CHUNK), first + ROUND, CHUNK):
                nc.scalar.activation(partners[:, c : c + CHUNK], table[:, c : c + CHUNK], IDENTITY)
            add_weighted_columns([table[:, first : first + ROUND]], [COUP_BLOCKS + first // BLOCK])
        nc.scalar.activation(partners[:, BANK:CHUNK], table[:, BANK:CHUNK], IDENTITY)

        def look_up(products, first, others):
            count = products.shape[1]
            picked = table[:].indirect(offsets[:, first // 16 : (first + count) // 16])
            nc.vector.tensor_tensor(products, picked, others, MULT)

        plain = []
        for look_ups in PLAIN_ROUNDS:
            parts = []
            for first, count in look_ups:
                products = held.tile([C, CHUNK + SUMS], F32, name=f"products_{first}")
                partner = first % S
                look_up(products[:, 0:count], first, partners[:, partner : partner + count])
                plain.append(products)
                parts.append(products[:, 0:count])
            add_weighted_columns(parts, [first // BLOCK for first, count in look_ups])
        weigh_waiting_round(True)

        latest = plain[-2][:, CHUNK - LATEST : CHUNK + SUMS]
        places = [plain[2][:, 0:BANK], plain[3][:, 0 : CHUNK - LATEST], latest[:, 0:LATEST]]
        for place, (first, count) in zip(places, WEIGHTED):
            at = first // S * CHUNK + first % S
            look_up(place, first, weighted_partners[:, at : at + count])

        def sum_products(u):
            nc.scalar.activation(
                plain[-1][:, 0 : places[u].shape[1]],
                places[u],
                IDENTITY,
                accum_out=latest[:, LATEST + u : LATEST + u + 1],
            )

        sum_products(0)
        partial_sb = held.tile([C, C], F32, name="partial_sb")
        nc.scalar.activation(partial_sb[:], partial[:], IDENTITY, bias=bias_column[:, 0:1])
        tensor_sum = psum.tile([C, 1], F32, name="tensor_sum")
        nc.tensor.matmul(tensor_sum[:], partial_sb[:], unit[:, 0:1], start=True, stop=True)
        sum_products(1)

        added = held.tile([C, LATEST + SUMS], F32, name="added")
        nc.vector.tensor_scalar(
            added[:], latest, 1.0, tensor_sum[:, 0:1], MULT, ADD, accum_out=energies[:, 0:1]
        )
        energy_rows = held.tile([C, SQUARE], F32, name="energy_rows", align_bytes=64)
        nc.vector.transpose(energy_rows[:], energies[:])
        nc.sync.dma_start(
            out.rearrange("(g r) o -> g (o r)", r=SQUARE), energy_rows[0:C:SQUARE, :]
        )
